import numpy as np
import ml_dtypes


def mxq(x, axis, fmt="e4m3"):
    dtype, down = {"e4m3": (ml_dtypes.float8_e4m3fn, 7), "e5m2": (ml_dtypes.float8_e5m2, 14)}[fmt]
    v = np.moveaxis(np.asarray(x, np.float32).astype(ml_dtypes.bfloat16).astype(np.float64), axis, -1)
    blocks = v.reshape(v.shape[:-1] + (-1, 32))
    amax = np.abs(blocks).max(-1, keepdims=True)
    byte = np.maximum(np.where(amax > 0, np.frexp(amax)[1] - 1 + 127, 0) - down, 1)
    scale = np.exp2(byte - 127.0)
    codes = (blocks / scale).astype(np.float32).astype(dtype).astype(np.float64)
    return np.moveaxis((codes * scale).reshape(v.shape), -1, axis)


WIDE = False


def mx_kscale(k):
    if not WIDE:
        return np.ones(k)
    levels = np.array([20, -20, 10, -10, 0])
    a = np.random.permutation(np.resize(levels, k // 512 * 4)).reshape(k // 512, 4)
    idx = np.arange(k)
    return np.exp2(a[idx // 512, idx % 128 // 32])


BF16 = ml_dtypes.bfloat16


def bf(x):
    return np.asarray(x, np.float32).astype(BF16)


def f64(x):
    return np.asarray(x).astype(np.float64)


B, C_IN, H, W, C_OUT = 2, 512, 64, 64, 512


def _box_sum(x):
    b, h, w, c = x.shape
    xp = np.pad(x, ((0, 0), (1, 1), (1, 1), (0, 0)))
    out = np.zeros_like(x)
    for i in range(3):
        for j in range(3):
            out = out + xp[:, i:i + h, j:j + w, :]
    return out


def setup_inputs():
    u = mx_kscale(C_OUT)
    x = np.random.standard_normal((B, C_IN, H, W))
    weight = np.random.standard_normal((1, C_IN, C_OUT)) * 3.0 / np.sqrt(C_IN) / u[None, None, :]
    g = (np.random.standard_normal((B, C_OUT, W, H))
         * np.exp2(np.random.randint(-12, 1, (B, 1, W, H))) * 4.0 * u[None, :, None, None])
    return {"x": bf(x), "weight": bf(weight), "grad_out": bf(g)}


def reference(x, weight, grad_out):
    g = f64(grad_out)
    wt = f64(weight)[0]
    b, c, h, w = np.shape(x)
    o = wt.shape[-1]
    g1 = np.transpose(g.reshape(b, o, h, w), (0, 2, 3, 1))
    gw = mxq(g1, 3, "e5m2") @ mxq(wt, 1, "e4m3").T
    deg = _box_sum(np.ones((1, h, w, 1)))
    dinv = 1.0 / np.sqrt(deg)
    gx = dinv * _box_sum(dinv * gw)
    return np.transpose(gx, (0, 3, 1, 2))

@@ -1,0 +1,356 @@
+from contextlib import ExitStack
+import math
+
+import concourse.mybir as mybir
+from concourse.masks import make_identity
+
+F32 = mybir.dt.float32
+BF16 = mybir.dt.bfloat16
+U32 = mybir.dt.uint32
+U8 = mybir.dt.uint8
+I32 = mybir.dt.int32
+E4X4 = mybir.dt.float8_e4m3fn_x4
+E5X4 = mybir.dt.float8_e5m2_x4
+ALU = mybir.AluOpType
+ACT = mybir.ActivationFunctionType
+
+P = 128
+B = 2
+C = 512
+SIDE = 64
+HALF = SIDE // 2
+PIX = SIDE * SIDE
+CHUNK_ROWS = 8
+CHUNK = CHUNK_ROWS * SIDE
+CHUNKS = PIX // CHUNK
+CT = C // P
+PADDED = PIX + 2 * SIDE
+
+FLOPS = 2 * B * PIX * C * C
+BYTES = B * C * PIX * 2 + C * C * 2 + B * C * PIX * 4
+
+U = math.sqrt(1.5)
+NINTH = 1.0 / 9.0
+
+UNITS = ((2, 2, 2, 2), (2, 2, 2, 1, 1))
+RAW_BUFS = 6
+
+
+def tile_gcn_layer_t_kernel(tc, x, weight, grad_out, out):
+    nc = tc.nc
+    with ExitStack() as ctx:
+        ctx.enter_context(tc.manual_schedule())
+        const = ctx.enter_context(tc.tile_pool(name="const", bufs=1))
+        raws = ctx.enter_context(tc.tile_pool(name="raws", bufs=RAW_BUFS))
+        grp = ctx.enter_context(tc.tile_pool(name="grp", bufs=4))
+        evens = ctx.enter_context(tc.tile_pool(name="evens", bufs=8))
+        small = ctx.enter_context(tc.tile_pool(name="small", bufs=4))
+        eds = ctx.enter_context(tc.tile_pool(name="eds", bufs=4))
+        outs = ctx.enter_context(tc.tile_pool(name="outs", bufs=5))
+        psum = ctx.enter_context(tc.psum_pool(name="psum", bufs=8))
+
+        g_flat = grad_out.rearrange("b (p t) i j -> b p t (i j)", t=4)
+        g_rows = grad_out.rearrange("b (p t) i j -> b p t i j", t=4)
+        out_v = out.rearrange("b (ct c) i j -> b c ct (i j)", c=P)
+
+        chunks = [("c", g // CHUNKS, g % CHUNKS) for g in range(B * CHUNKS)]
+        prep = chunks[0:2] + [("e", 0, 0)] + chunks[2:]
+        main = chunks[0:1] + [("e", 0, 0)] + chunks[1:14] + [chunks[15], chunks[14]]
+        n_items = len(main)
+        unit_of = {}
+        for b in range(B):
+            k0 = 0
+            for n in UNITS[b]:
+                for k in range(k0, k0 + n):
+                    unit_of[(b, k)] = (k0, n)
+                k0 += n
+
+        pieces = [("w", 0, 0, 1), ("c", 0, 0, 1), ("c", 0, 1, 1), ("e", 0, 0, 1)]
+        pieces += [("c", 0, k, 2) for k in (2, 4, 6)] + [("c", 1, k, 2) for k in (0, 2, 4, 6)]
+        src = {}
+        owner = {}
+        left = {}
+        ring = {"next": 0, "in_use": 0}
+
+        def pump():
+            while ring["next"] < len(pieces) and ring["in_use"] < RAW_BUFS:
+                n = ring["next"]
+                kind, b, k0, nk = pieces[n]
+                left[n] = nk
+                if kind == "w":
+                    raw = raws.tile([P, CT, C], BF16, tag="raw", name="raw%d" % n)
+                    nc.sync.dma_start(out=raw[:], in_=weight[0].rearrange("(ct c) o -> c ct o", c=P))
+                    src["w"] = raw[:]
+                    owner["w"] = n
+                elif kind == "e":
+                    raw = raws.tile([P, 4, 4, SIDE], BF16, tag="raw", name="raw%d" % n)
+                    for bb in range(B):
+                        for e in range(2):
+                            nc.sync.dma_start(out=raw[:, :, 2 * bb + e, :], in_=g_rows[bb, :, :, e * (SIDE - 1), :])
+                    src["e"] = raw[:].rearrange("p t r j -> p t (r j)")
+                    owner["e"] = n
+                else:
+                    raw = raws.tile([P, 4, nk * CHUNK], BF16, tag="raw", name="raw%d" % n)
+                    nc.sync.dma_start(out=raw[:], in_=g_flat[b, :, :, k0 * CHUNK : (k0 + nk) * CHUNK])
+                    for i in range(nk):
+                        src[(b, k0 + i)] = raw[:, :, i * CHUNK : (i + 1) * CHUNK]
+                        owner[(b, k0 + i)] = n
+                ring["next"] = n + 1
+                ring["in_use"] = ring["in_use"] + 1
+
+        def release(key):
+            n = owner[key]
+            left[n] = left[n] - 1
+            if left[n] == 0:
+                ring["in_use"] = ring["in_use"] - 1
+                pump()
+
+        pump()
+
+        ident = const.tile([P, P], F32)
+        make_identity(nc, ident[:])
+        codes = const.tile([P, B, PADDED], U32, align_bytes=64)
+        scales = const.tile([P, B, PADDED], U8, align_bytes=64)
+        e_codes = const.tile([P, CHUNK], U32, align_bytes=64)
+        e_scales = const.tile([P, CHUNK], U8, align_bytes=64)
+        w_codes = const.tile([P, C], U32, align_bytes=64)
+        w_scales = const.tile([P, C], U8, align_bytes=64)
+        extra = const.tile([P, CT, 4 * SIDE], F32)
+        nc.vector.memset(codes[:, :, 0:SIDE].bitcast(I32), 0)
+        nc.vector.memset(codes[:, :, PADDED - SIDE : PADDED].bitcast(I32), 0)
+        nc.vector.memset(scales[:, :, 0:SIDE].bitcast(I32), 0)
+        nc.vector.memset(scales[:, :, PADDED - SIDE : PADDED].bitcast(I32), 0)
+        nc.vector.memset(e_codes[:, 4 * SIDE : CHUNK].bitcast(I32), 0)
+        nc.vector.memset(e_scales[:, 4 * SIDE : CHUNK].bitcast(I32), 0)
+
+        def regroup(copy, src_ap, dst_ap):
+            copy(
+                out=dst_ap.rearrange("p (a s t) -> p a t s", s=2, t=4),
+                in_=src_ap.rearrange("p t (a s) -> p a t s", s=2)[:, :, :, ::-1],
+            )
+
+        grouped_w = grp.tile([P, 4 * C], BF16, align_bytes=64, tag="grouped", name="grouped_w")
+        w32 = src["w"].bitcast(F32)
+        gw32 = grouped_w[:].bitcast(F32).rearrange("p (ct c h) -> p ct c h", ct=CT, h=2)
+        for half in range(2):
+            w_t = psum.tile([P, CHUNK], F32, tag="bank", name="w_t%d" % half)
+            w_tv = w_t[:].rearrange("p (c2 h c) -> p c2 h c", c2=2, h=2)
+            for c2 in range(2):
+                for h in range(2):
+                    nc.tensor.transpose(w_tv[:, c2, h, :], w32[:, 2 * half + c2, h : C // 2 : 2], ident[:])
+            nc.scalar.copy(out=gw32[:, 2 * half : 2 * half + 2, :, :], in_=w_tv.rearrange("p c2 h c -> p c2 c h"))
+        release("w")
+
+        def multiply(bank, ct, windows):
+            for n, (rhs, rhs_scale) in enumerate(windows):
+                nc.tensor.matmul_mx(
+                    out=bank[:],
+                    lhsT=w_codes[:, ct * P : (ct + 1) * P].bitcast(E4X4),
+                    lhsT_scale=w_scales[:, ct * P : (ct + 1) * P],
+                    rhs=rhs.bitcast(E5X4),
+                    rhs_scale=rhs_scale,
+                    start=(n == 0),
+                    stop=(n == len(windows) - 1),
+                )
+
+        def column_edges(on_vector, rows, o3, ed3):
+            edge = ed3[:, :, 1:3]
+            inner = ed3[:, :, 0:4:3]
+            next_cols = o3[:, :, 1 : SIDE - 1 : SIDE - 3]
+            edge_cols = o3[:, :, 0 : SIDE : SIDE - 1]
+            if on_vector:
+                nc.vector.scalar_tensor_tensor(
+                    out=next_cols, in0=edge, scalar=(U - 1.0) / U, in1=next_cols, op0=ALU.mult, op1=ALU.add
+                )
+                nc.vector.scalar_tensor_tensor(out=edge_cols, in0=edge, scalar=U, in1=inner, op0=ALU.mult, op1=ALU.add)
+            else:
+                t1 = small.tile([P, rows, 2], F32, tag="t1")
+                t2 = small.tile([P, rows, 2], F32, tag="t2")
+                nc.gpsimd.tensor_scalar(
+                    out=t1[:], in0=edge, scalar1=(U - 1.0) / U, scalar2=0.0, op0=ALU.mult, op1=ALU.add
+                )
+                nc.gpsimd.tensor_scalar(out=t2[:], in0=edge, scalar1=U, scalar2=0.0, op0=ALU.mult, op1=ALU.add)
+                nc.gpsimd.tensor_tensor(out=next_cols, in0=next_cols, in1=t1[:], op=ALU.add)
+                nc.gpsimd.tensor_tensor(out=edge_cols, in0=t2[:], in1=inner, op=ALU.add)
+
+        extra4 = extra[:].rearrange("p ct (r j) -> p ct r j", j=SIDE)
+
+        def row_edge(o4, first, edge_row, which):
+            two = o4[:, :, first : first + 2, :]
+            nc.gpsimd.tensor_tensor(
+                out=two, in0=two, in1=extra4[:, :, which, :].unsqueeze(2).to_broadcast([P, CT, 2, SIDE]), op=ALU.add
+            )
+            nc.gpsimd.tensor_scalar(
+                out=o4[:, :, edge_row, :], in0=o4[:, :, edge_row, :], scalar1=U, scalar2=0.0, op0=ALU.mult, op1=ALU.add
+            )
+
+        grouped_of = {}
+        work = {}
+        unit_tiles = {}
+
+        def geometry(item):
+            kind, b, k = item
+            if kind == "e":
+                return 4 * SIDE, (U - 1.0) * NINTH, 0, 0, 1
+            k0, n = unit_of[(b, k)]
+            return CHUNK, NINTH, (k - k0), k0, n
+
+        def stage_a(item, copy):
+            kind, b, k = item
+            key = "e" if kind == "e" else (b, k)
+            width = geometry(item)[0]
+            grouped = grp.tile([P, 4 * CHUNK], BF16, align_bytes=64, tag="grouped", name="grouped_%s%d_%d" % item)
+            regroup(copy, src[key], grouped[:, 0 : 4 * width])
+            grouped_of[item] = grouped
+            release(key)
+
+        def stage_q(item):
+            kind, b, k = item
+            grouped = grouped_of[item]
+            if kind == "e":
+                nc.vector.quantize_mx(
+                    out=e_codes[:, 0 : 4 * SIDE].bitcast(E5X4),
+                    scales=e_scales[:, 0 : 4 * SIDE],
+                    in_=grouped[:, 0 : 16 * SIDE],
+                )
+            else:
+                c0 = SIDE + k * CHUNK
+                nc.vector.quantize_mx(
+                    out=codes[:, b, c0 : c0 + CHUNK].bitcast(E5X4), scales=scales[:, b, c0 : c0 + CHUNK], in_=grouped[:]
+                )
+
+        def stage_m(item, ct):
+            kind, b, k = item
+            bank = psum.tile([P, CHUNK], F32, tag="bank", name="bank_%s%d_%d_%d" % (kind, b, k, ct))
+            if kind == "e":
+                multiply(bank, ct, [(e_codes[:], e_scales[:])])
+            else:
+                windows = []
+                for d in (-1, 0, 1):
+                    c0 = SIDE + k * CHUNK + d * SIDE
+                    windows.append((codes[:, b, c0 : c0 + CHUNK], scales[:, b, c0 : c0 + CHUNK]))
+                multiply(bank, ct, windows)
+            work[(item, ct)] = [bank, None, None]
+
+        def stage_e(item, ct):
+            kind, b, k = item
+            width, c, part, k0, n = geometry(item)
+            ukey = (kind, b, k0)
+            if part == 0 and ct == 0:
+                ed_new = eds.tile([P, CT, n * width // SIDE, 4], F32, tag="ed", name="ed_%s%d_%d" % item)
+                unit_tiles[ukey] = [ed_new, None]
+            ed = unit_tiles[ukey][0]
+            rows = width // SIDE
+            xv = work[(item, ct)][0][:, 0:width]
+            nc.scalar.activation(
+                out=ed[:, ct, part * rows : (part + 1) * rows, :].rearrange("p r (s k) -> p r s k", k=2),
+                in_=xv.rearrange("p (r s k) -> p r s k", s=HALF, k=2)[:, :, 0 : HALF : HALF - 1, :],
+                func=ACT.Copy,
+                scale=U * c,
+            )
+            even = evens.tile([P, CHUNK // 2], F32, tag="even", name="even_%s%d_%d_%d" % (kind, b, k, ct))
+            nc.scalar.activation(out=even[:, 0 : width // 2], in_=xv[:, 1:width:2], func=ACT.Copy, scale=c)
+            work[(item, ct)][1] = even
+
+        def stage_p(item, ct):
+            width, c, part, k0, n = geometry(item)
+            bank, even, unused = work[(item, ct)]
+            m = width // 2 - 1
+            pair = small.tile([P, CHUNK // 2], F32, tag="pair", name="pair_%s%d_%d_%d" % (item[0], item[1], item[2], ct))
+            nc.vector.scalar_tensor_tensor(
+                out=pair[:, 0:m],
+                in0=bank[:, 0 : width - 2 : 2],
+                scalar=c,
+                in1=even[:, 1 : width // 2],
+                op0=ALU.mult,
+                op1=ALU.add,
+            )
+            work[(item, ct)][2] = pair
+
+        def out_tile(item):
+            kind, b, k = item
+            width, c, part, k0, n = geometry(item)
+            if kind == "e":
+                return extra
+            ukey = (kind, b, k0)
+            if unit_tiles[ukey][1] is None:
+                unit_tiles[ukey][1] = outs.tile([P, CT, n * CHUNK], F32, tag="o", name="o_%d_%d" % (b, k0))
+            return unit_tiles[ukey][1]
+
+        def stage_h(item, ct):
+            width, c, part, k0, n = geometry(item)
+            bank, even, pair = work[(item, ct)]
+            m = width // 2 - 1
+            o_flat = out_tile(item)[:, ct, part * width : (part + 1) * width]
+            nc.vector.scalar_tensor_tensor(
+                out=o_flat[:, 1 : width - 1].rearrange("p (m e) -> p m e", e=2),
+                in0=bank[:, 1 : width - 1].rearrange("p (m e) -> p m e", e=2),
+                scalar=c,
+                in1=pair[:, 0:m].unsqueeze(2).to_broadcast([P, m, 2]),
+                op0=ALU.mult,
+                op1=ALU.add,
+            )
+
+        def finish_unit(item):
+            kind, b, k = item
+            width, c, part, k0, n = geometry(item)
+            if part != n - 1:
+                return
+            o_t = out_tile(item)
+            ed = unit_tiles[(kind, b, k0)][0]
+            rows = n * width // SIDE
+            column_edges(
+                False,
+                CT * rows,
+                o_t[:].rearrange("p ct (r j) -> p (ct r) j", j=SIDE),
+                ed[:].rearrange("p ct r k -> p (ct r) k"),
+            )
+            if kind == "e":
+                return
+            o4 = o_t[:].rearrange("p ct (r j) -> p ct r j", j=SIDE)
+            if k0 == 0:
+                row_edge(o4, 0, 0, 2 * b)
+            if k == CHUNKS - 1:
+                row_edge(o4, rows - 2, rows - 1, 2 * b + 1)
+            nc.sync.dma_start(out=out_v[b, :, :, k0 * CHUNK : (k0 + n) * CHUNK], in_=o_t[:])
+
+        def finish_last(item, ct):
+            kind, b, k = item
+            o_t = out_tile(item)
+            ed = unit_tiles[(kind, b, k)][0]
+            column_edges(True, CHUNK_ROWS, o_t[:, ct, :].rearrange("p (r j) -> p r j", j=SIDE), ed[:, ct, :, :])
+            nc.sync.dma_start(out=out_v[b, :, ct, k * CHUNK : (k + 1) * CHUNK], in_=o_t[:, ct, :])
+
+        stage_a(prep[0], nc.vector.tensor_copy)
+        stage_a(prep[1], nc.vector.tensor_copy)
+        stage_a(prep[2], nc.scalar.copy)
+        stage_q(prep[0])
+        nc.vector.quantize_mx(out=w_codes[:].bitcast(E4X4), scales=w_scales[:], in_=grouped_w[:])
+        stage_q(prep[1])
+        stage_q(prep[2])
+        for i in range(-1, n_items):
+            if i + 1 < n_items:
+                for ct in range(CT):
+                    stage_m(main[i + 1], ct)
+                    stage_e(main[i + 1], ct)
+            if i + 4 < n_items:
+                stage_a(prep[i + 4], nc.scalar.copy)
+            if i == -1:
+                stage_p(main[0], 0)
+            if i >= 0:
+                last = i == n_items - 1
+                for ct in range(CT):
+                    if ct < CT - 1:
+                        stage_p(main[i], ct + 1)
+                    else:
+                        if i + 3 < n_items:
+                            stage_q(prep[i + 3])
+                        if i + 1 < n_items:
+                            stage_p(main[i + 1], 0)
+                    stage_h(main[i], ct)
+                    if last and ct > 0:
+                        finish_last(main[i], ct - 1)
+                if last:
+                    finish_last(main[i], CT - 1)
+                else:
+                    finish_unit(main[i])

@@ -32,7 +32,7 @@ BYTES = B * C * PIX * 2 + C * C * 2 + B * C * PIX * 4
 U = math.sqrt(1.5)
 NINTH = 1.0 / 9.0
 
-UNITS = ((2, 2, 2, 2), (2, 2, 2, 1, 1))
+UNITS = ((2, 2, 2, 2), (2, 2, 1, 1, 1, 1))
 RAW_BUFS = 6
 
 
@@ -42,7 +42,7 @@ def tile_gcn_layer_t_kernel(tc, x, weight, grad_out, out):
         ctx.enter_context(tc.manual_schedule())
         const = ctx.enter_context(tc.tile_pool(name="const", bufs=1))
         raws = ctx.enter_context(tc.tile_pool(name="raws", bufs=RAW_BUFS))
-        grp = ctx.enter_context(tc.tile_pool(name="grp", bufs=4))
+        grp = ctx.enter_context(tc.tile_pool(name="grp", bufs=5))
         evens = ctx.enter_context(tc.tile_pool(name="evens", bufs=8))
         small = ctx.enter_context(tc.tile_pool(name="small", bufs=4))
         eds = ctx.enter_context(tc.tile_pool(name="eds", bufs=4))
@@ -55,7 +55,7 @@ def tile_gcn_layer_t_kernel(tc, x, weight, grad_out, out):
 
         chunks = [("c", g // CHUNKS, g % CHUNKS) for g in range(B * CHUNKS)]
         prep = chunks[0:2] + [("e", 0, 0)] + chunks[2:]
-        main = chunks[0:1] + [("e", 0, 0)] + chunks[1:14] + [chunks[15], chunks[14]]
+        main = chunks[0:1] + [("e", 0, 0)] + chunks[1:13] + [chunks[15], chunks[13], chunks[14]]
         n_items = len(main)
         unit_of = {}
         for b in range(B):
@@ -65,8 +65,8 @@ def tile_gcn_layer_t_kernel(tc, x, weight, grad_out, out):
                     unit_of[(b, k)] = (k0, n)
                 k0 += n
 
-        pieces = [("w", 0, 0, 1), ("c", 0, 0, 1), ("c", 0, 1, 1), ("e", 0, 0, 1)]
-        pieces += [("c", 0, k, 2) for k in (2, 4, 6)] + [("c", 1, k, 2) for k in (0, 2, 4, 6)]
+        pieces = [("c", 0, 0, 1), ("w", 0, 0, 1), ("c", 0, 1, 1), ("e", 0, 0, 1), ("c", 0, 2, 1), ("c", 0, 3, 1)]
+        pieces += [("c", 0, k, 2) for k in (4, 6)] + [("c", 1, k, 2) for k in (0, 2, 4, 6)]
         src = {}
         owner = {}
         left = {}
@@ -204,8 +204,11 @@ def tile_gcn_layer_t_kernel(tc, x, weight, grad_out, out):
             grouped_of[item] = grouped
             release(key)
 
+        done_q = []
+
         def stage_q(item):
             kind, b, k = item
+            done_q.append(item)
             grouped = grouped_of[item]
             if kind == "e":
                 nc.vector.quantize_mx(
@@ -222,6 +225,9 @@ def tile_gcn_layer_t_kernel(tc, x, weight, grad_out, out):
         def stage_m(item, ct):
             kind, b, k = item
             bank = psum.tile([P, CHUNK], F32, tag="bank", name="bank_%s%d_%d_%d" % (kind, b, k, ct))
+            assert item in done_q
+            assert kind == "e" or k == 0 or ("c", b, k - 1) in done_q
+            assert kind == "e" or k == CHUNKS - 1 or ("c", b, k + 1) in done_q
             if kind == "e":
                 multiply(bank, ct, [(e_codes[:], e_scales[:])])
             else:
@@ -322,34 +328,39 @@ def tile_gcn_layer_t_kernel(tc, x, weight, grad_out, out):
             nc.sync.dma_start(out=out_v[b, :, ct, k * CHUNK : (k + 1) * CHUNK], in_=o_t[:, ct, :])
 
         stage_a(prep[0], nc.vector.tensor_copy)
+        stage_q(prep[0])
         stage_a(prep[1], nc.vector.tensor_copy)
         stage_a(prep[2], nc.scalar.copy)
-        stage_q(prep[0])
         nc.vector.quantize_mx(out=w_codes[:].bitcast(E4X4), scales=w_scales[:], in_=grouped_w[:])
         stage_q(prep[1])
         stage_q(prep[2])
+        stage_a(prep[3], nc.vector.tensor_copy)
         for i in range(-1, n_items):
             if i + 1 < n_items:
                 for ct in range(CT):
                     stage_m(main[i + 1], ct)
                     stage_e(main[i + 1], ct)
-            if i + 4 < n_items:
-                stage_a(prep[i + 4], nc.scalar.copy)
-            if i == -1:
-                stage_p(main[0], 0)
+            if i + 5 < n_items:
+                stage_a(prep[i + 5], nc.scalar.copy)
+            last = i == n_items - 1
+            banks = []
             if i >= 0:
-                last = i == n_items - 1
-                for ct in range(CT):
-                    if ct < CT - 1:
-                        stage_p(main[i], ct + 1)
-                    else:
-                        if i + 3 < n_items:
-                            stage_q(prep[i + 3])
-                        if i + 1 < n_items:
-                            stage_p(main[i + 1], 0)
-                    stage_h(main[i], ct)
-                    if last and ct > 0:
-                        finish_last(main[i], ct - 1)
+                banks = list(range(CT))
+            for n in range(len(banks) + 1):
+                if n + 1 < len(banks):
+                    stage_p(main[i], banks[n + 1])
+                if n + 1 == max(len(banks), 1):
+                    if i >= 0 and i + 3 < n_items - 1:
+                        stage_q(prep[i + 3])
+                    if i + 3 == n_items - 2:
+                        stage_q(prep[i + 4])
+                    if i + 1 < n_items:
+                        stage_p(main[i + 1], 0)
+                if n < len(banks):
+                    stage_h(main[i], banks[n])
+                    if last and n > 0:
+                        finish_last(main[i], banks[n - 1])
+            if i >= 0:
                 if last:
                     finish_last(main[i], CT - 1)
                 else:

@@ -34,6 +34,7 @@ NINTH = 1.0 / 9.0
 
 UNITS = ((2, 2, 2, 2), (2, 2, 1, 1, 1, 1))
 RAW_BUFS = 6
+HALVED = 2
 
 
 def tile_gcn_layer_t_kernel(tc, x, weight, grad_out, out):
@@ -65,7 +66,7 @@ def tile_gcn_layer_t_kernel(tc, x, weight, grad_out, out):
                     unit_of[(b, k)] = (k0, n)
                 k0 += n
 
-        pieces = [("c", 0, 0, 1), ("w", 0, 0, 1), ("c", 0, 1, 1), ("e", 0, 0, 1), ("c", 0, 2, 1), ("c", 0, 3, 1)]
+        pieces = [("c", 0, 0, 1), ("w", 0, 0, 1), ("c", 0, 1, 1), ("w", 0, 2, 1), ("e", 0, 0, 1), ("c", 0, 2, 1), ("c", 0, 3, 1)]
         pieces += [("c", 0, k, 2) for k in (4, 6)] + [("c", 1, k, 2) for k in (0, 2, 4, 6)]
         src = {}
         owner = {}
@@ -78,10 +79,16 @@ def tile_gcn_layer_t_kernel(tc, x, weight, grad_out, out):
                 kind, b, k0, nk = pieces[n]
                 left[n] = nk
                 if kind == "w":
-                    raw = raws.tile([P, CT, C], BF16, tag="raw", name="raw%d" % n)
-                    nc.sync.dma_start(out=raw[:], in_=weight[0].rearrange("(ct c) o -> c ct o", c=P))
-                    src["w"] = raw[:]
-                    owner["w"] = n
+                    if k0 == 0:
+                        raw = raws.tile([P, CT, C], BF16, tag="raw", name="raw%d" % n)
+                        src["w"] = raw[:]
+                        owner["w"] = n
+                    else:
+                        ring["in_use"] = ring["in_use"] - 1
+                    nc.sync.dma_start(
+                        out=src["w"][:, k0 : k0 + 2, :],
+                        in_=weight[0].rearrange("(ct c) o -> c ct o", c=P)[:, k0 : k0 + 2, :],
+                    )
                 elif kind == "e":
                     raw = raws.tile([P, 4, 4, SIDE], BF16, tag="raw", name="raw%d" % n)
                     for bb in range(B):
@@ -175,10 +182,13 @@ def tile_gcn_layer_t_kernel(tc, x, weight, grad_out, out):
 
         extra4 = extra[:].rearrange("p ct (r j) -> p ct r j", j=SIDE)
 
-        def row_edge(o4, first, edge_row, which):
+        def row_edge(o4, first, edge_row, which, ct0=0, nct=CT):
             two = o4[:, :, first : first + 2, :]
             nc.gpsimd.tensor_tensor(
-                out=two, in0=two, in1=extra4[:, :, which, :].unsqueeze(2).to_broadcast([P, CT, 2, SIDE]), op=ALU.add
+                out=two,
+                in0=two,
+                in1=extra4[:, ct0 : ct0 + nct, which, :].unsqueeze(2).to_broadcast([P, nct, 2, SIDE]),
+                op=ALU.add,
             )
             nc.gpsimd.tensor_scalar(
                 out=o4[:, :, edge_row, :], in0=o4[:, :, edge_row, :], scalar1=U, scalar2=0.0, op0=ALU.mult, op1=ALU.add
@@ -320,6 +330,20 @@ def tile_gcn_layer_t_kernel(tc, x, weight, grad_out, out):
                 row_edge(o4, rows - 2, rows - 1, 2 * b + 1)
             nc.sync.dma_start(out=out_v[b, :, :, k0 * CHUNK : (k0 + n) * CHUNK], in_=o_t[:])
 
+        def finish_half(item, ct0):
+            kind, b, k = item
+            o_t = out_tile(item)[:, ct0 : ct0 + 2, :]
+            ed = unit_tiles[(kind, b, k)][0][:, ct0 : ct0 + 2, :, :]
+            column_edges(
+                False,
+                2 * CHUNK_ROWS,
+                o_t.rearrange("p ct (r j) -> p (ct r) j", j=SIDE),
+                ed.rearrange("p ct r k -> p (ct r) k"),
+            )
+            if k == CHUNKS - 1:
+                row_edge(o_t.rearrange("p ct (r j) -> p ct r j", j=SIDE), CHUNK_ROWS - 2, CHUNK_ROWS - 1, 2 * b + 1, ct0, 2)
+            nc.sync.dma_start(out=out_v[b, :, ct0 : ct0 + 2, k * CHUNK : (k + 1) * CHUNK], in_=o_t)
+
         def finish_last(item, ct):
             kind, b, k = item
             o_t = out_tile(item)
@@ -327,12 +351,20 @@ def tile_gcn_layer_t_kernel(tc, x, weight, grad_out, out):
             column_edges(True, CHUNK_ROWS, o_t[:, ct, :].rearrange("p (r j) -> p r j", j=SIDE), ed[:, ct, :, :])
             nc.sync.dma_start(out=out_v[b, :, ct, k * CHUNK : (k + 1) * CHUNK], in_=o_t[:, ct, :])
 
+        def quantise_w(half):
+            nc.vector.quantize_mx(
+                out=w_codes[:, half * 2 * P : (half + 1) * 2 * P].bitcast(E4X4),
+                scales=w_scales[:, half * 2 * P : (half + 1) * 2 * P],
+                in_=grouped_w[:, half * 2 * C : (half + 1) * 2 * C],
+            )
+
         stage_a(prep[0], nc.vector.tensor_copy)
         stage_q(prep[0])
+        quantise_w(0)
         stage_a(prep[1], nc.vector.tensor_copy)
         stage_a(prep[2], nc.scalar.copy)
-        nc.vector.quantize_mx(out=w_codes[:].bitcast(E4X4), scales=w_scales[:], in_=grouped_w[:])
         stage_q(prep[1])
+        quantise_w(1)
         stage_q(prep[2])
         stage_a(prep[3], nc.vector.tensor_copy)
         for i in range(-1, n_items):
@@ -343,6 +375,7 @@ def tile_gcn_layer_t_kernel(tc, x, weight, grad_out, out):
             if i + 5 < n_items:
                 stage_a(prep[i + 5], nc.scalar.copy)
             last = i == n_items - 1
+            halves = n_items - 1 - HALVED <= i < n_items - 1
             banks = []
             if i >= 0:
                 banks = list(range(CT))
@@ -360,8 +393,10 @@ def tile_gcn_layer_t_kernel(tc, x, weight, grad_out, out):
                     stage_h(main[i], banks[n])
                     if last and n > 0:
                         finish_last(main[i], banks[n - 1])
+                    if halves and n % 2 == 1:
+                        finish_half(main[i], n - 1)
             if i >= 0:
                 if last:
                     finish_last(main[i], CT - 1)
-                else:
+                elif not halves:
                     finish_unit(main[i])

@@ -34,6 +34,7 @@ NINTH = 1.0 / 9.0
 
 UNITS = ((2, 2, 2, 2), (2, 2, 1, 1, 1, 1))
 RAW_BUFS = 6
+G_COLS = 128
 HALVED = 2
 
 
@@ -43,7 +44,7 @@ def tile_gcn_layer_t_kernel(tc, x, weight, grad_out, out):
         ctx.enter_context(tc.manual_schedule())
         const = ctx.enter_context(tc.tile_pool(name="const", bufs=1))
         raws = ctx.enter_context(tc.tile_pool(name="raws", bufs=RAW_BUFS))
-        grp = ctx.enter_context(tc.tile_pool(name="grp", bufs=5))
+        grp = ctx.enter_context(tc.tile_pool(name="grp", bufs=3))
         evens = ctx.enter_context(tc.tile_pool(name="evens", bufs=8))
         small = ctx.enter_context(tc.tile_pool(name="small", bufs=4))
         eds = ctx.enter_context(tc.tile_pool(name="eds", bufs=4))
@@ -136,7 +137,7 @@ def tile_gcn_layer_t_kernel(tc, x, weight, grad_out, out):
                 in_=src_ap.rearrange("p t (a s) -> p a t s", s=2)[:, :, :, ::-1],
             )
 
-        grouped_w = grp.tile([P, 4 * C], BF16, align_bytes=64, tag="grouped", name="grouped_w")
+        grouped_w = const.tile([P, 4 * C], BF16, align_bytes=64, name="grouped_w")
         w32 = src["w"].bitcast(F32)
         gw32 = grouped_w[:].bitcast(F32).rearrange("p (ct c h) -> p ct c h", ct=CT, h=2)
         for half in range(2):
@@ -215,6 +216,21 @@ def tile_gcn_layer_t_kernel(tc, x, weight, grad_out, out):
             release(key)
 
         done_q = []
+
+        def stage_a_shared(item):
+            kind, b, k = item
+            grouped = grp.tile([P, 4 * CHUNK], BF16, align_bytes=64, tag="grouped", name="grouped_%s%d_%d" % item)
+            nc.gpsimd.tensor_scalar(
+                out=grouped[:, 0 : 4 * G_COLS].rearrange("p (a s t) -> p a s t", s=2, t=4),
+                in0=src[(b, k)][:, :, 0:G_COLS].rearrange("p t (a s) -> p a s t", s=2)[:, :, ::-1, :],
+                scalar1=1.0,
+                scalar2=0.0,
+                op0=ALU.mult,
+                op1=ALU.add,
+            )
+            regroup(nc.scalar.copy, src[(b, k)][:, :, G_COLS:CHUNK], grouped[:, 4 * G_COLS : 4 * CHUNK])
+            grouped_of[item] = grouped
+            release((b, k))
 
         def stage_q(item):
             kind, b, k = item
@@ -373,7 +389,7 @@ def tile_gcn_layer_t_kernel(tc, x, weight, grad_out, out):
                     stage_m(main[i + 1], ct)
                     stage_e(main[i + 1], ct)
             if i + 5 < n_items:
-                stage_a(prep[i + 5], nc.scalar.copy)
+                stage_a_shared(prep[i + 5])
             last = i == n_items - 1
             halves = n_items - 1 - HALVED <= i < n_items - 1
             banks = []

@@ -140,14 +140,13 @@ def tile_gcn_layer_t_kernel(tc, x, weight, grad_out, out):
         grouped_w = const.tile([P, 4 * C], BF16, align_bytes=64, name="grouped_w")
         w32 = src["w"].bitcast(F32)
         gw32 = grouped_w[:].bitcast(F32).rearrange("p (ct c h) -> p ct c h", ct=CT, h=2)
-        for half in range(2):
+        def transpose_w(half):
             w_t = psum.tile([P, CHUNK], F32, tag="bank", name="w_t%d" % half)
             w_tv = w_t[:].rearrange("p (c2 h c) -> p c2 h c", c2=2, h=2)
             for c2 in range(2):
                 for h in range(2):
                     nc.tensor.transpose(w_tv[:, c2, h, :], w32[:, 2 * half + c2, h : C // 2 : 2], ident[:])
             nc.scalar.copy(out=gw32[:, 2 * half : 2 * half + 2, :, :], in_=w_tv.rearrange("p c2 h c -> p c2 c h"))
-        release("w")
 
         def multiply(bank, ct, windows):
             for n, (rhs, rhs_scale) in enumerate(windows):
@@ -216,6 +215,14 @@ def tile_gcn_layer_t_kernel(tc, x, weight, grad_out, out):
             release(key)
 
         done_q = []
+
+        def stage_a_split(item, v_cols):
+            kind, b, k = item
+            grouped = grp.tile([P, 4 * CHUNK], BF16, align_bytes=64, tag="grouped", name="grouped_%s%d_%d" % item)
+            regroup(nc.vector.tensor_copy, src[(b, k)][:, :, 0:v_cols], grouped[:, 0 : 4 * v_cols])
+            regroup(nc.scalar.copy, src[(b, k)][:, :, v_cols:CHUNK], grouped[:, 4 * v_cols : 4 * CHUNK])
+            grouped_of[item] = grouped
+            release((b, k))
 
         def stage_a_shared(item):
             kind, b, k = item
@@ -374,15 +381,18 @@ def tile_gcn_layer_t_kernel(tc, x, weight, grad_out, out):
                 in_=grouped_w[:, half * 2 * C : (half + 1) * 2 * C],
             )
 
-        stage_a(prep[0], nc.vector.tensor_copy)
+        stage_a_split(prep[0], 352)
+        transpose_w(0)
         stage_q(prep[0])
         quantise_w(0)
-        stage_a(prep[1], nc.vector.tensor_copy)
+        stage_a_split(prep[1], 352)
+        transpose_w(1)
+        release("w")
         stage_a(prep[2], nc.scalar.copy)
         stage_q(prep[1])
         quantise_w(1)
         stage_q(prep[2])
-        stage_a(prep[3], nc.vector.tensor_copy)
+        stage_a_split(prep[3], 352)
         for i in range(-1, n_items):
             if i + 1 < n_items:
                 for ct in range(CT):

@@ -33,7 +33,6 @@ U = math.sqrt(1.5)
 NINTH = 1.0 / 9.0
 
 UNITS = ((2, 2, 2, 2), (2, 2, 1, 1, 1, 1))
-RAW_BUFS = 6
 G_COLS = 128
 HALVED = 2
 
@@ -43,7 +42,7 @@ def tile_gcn_layer_t_kernel(tc, x, weight, grad_out, out):
     with ExitStack() as ctx:
         ctx.enter_context(tc.manual_schedule())
         const = ctx.enter_context(tc.tile_pool(name="const", bufs=1))
-        raws = ctx.enter_context(tc.tile_pool(name="raws", bufs=RAW_BUFS))
+        raws = ctx.enter_context(tc.tile_pool(name="raws", bufs=1))
         grp = ctx.enter_context(tc.tile_pool(name="grp", bufs=3))
         evens = ctx.enter_context(tc.tile_pool(name="evens", bufs=8))
         small = ctx.enter_context(tc.tile_pool(name="small", bufs=4))
@@ -70,50 +69,25 @@ def tile_gcn_layer_t_kernel(tc, x, weight, grad_out, out):
         pieces = [("c", 0, 0, 1), ("w", 0, 0, 1), ("c", 0, 1, 1), ("w", 0, 2, 1), ("e", 0, 0, 1), ("c", 0, 2, 1), ("c", 0, 3, 1)]
         pieces += [("c", 0, k, 2) for k in (4, 6)] + [("c", 1, k, 2) for k in (0, 2, 4, 6)]
         src = {}
-        owner = {}
-        left = {}
-        ring = {"next": 0, "in_use": 0}
-
-        def pump():
-            while ring["next"] < len(pieces) and ring["in_use"] < RAW_BUFS:
-                n = ring["next"]
-                kind, b, k0, nk = pieces[n]
-                left[n] = nk
-                if kind == "w":
-                    if k0 == 0:
-                        raw = raws.tile([P, CT, C], BF16, tag="raw", name="raw%d" % n)
-                        src["w"] = raw[:]
-                        owner["w"] = n
-                    else:
-                        ring["in_use"] = ring["in_use"] - 1
-                    nc.sync.dma_start(
-                        out=src["w"][:, k0 : k0 + 2, :],
-                        in_=weight[0].rearrange("(ct c) o -> c ct o", c=P)[:, k0 : k0 + 2, :],
-                    )
-                elif kind == "e":
-                    raw = raws.tile([P, 4, 4, SIDE], BF16, tag="raw", name="raw%d" % n)
-                    for bb in range(B):
-                        for e in range(2):
-                            nc.sync.dma_start(out=raw[:, :, 2 * bb + e, :], in_=g_rows[bb, :, :, e * (SIDE - 1), :])
-                    src["e"] = raw[:].rearrange("p t r j -> p t (r j)")
-                    owner["e"] = n
-                else:
-                    raw = raws.tile([P, 4, nk * CHUNK], BF16, tag="raw", name="raw%d" % n)
-                    nc.sync.dma_start(out=raw[:], in_=g_flat[b, :, :, k0 * CHUNK : (k0 + nk) * CHUNK])
-                    for i in range(nk):
-                        src[(b, k0 + i)] = raw[:, :, i * CHUNK : (i + 1) * CHUNK]
-                        owner[(b, k0 + i)] = n
-                ring["next"] = n + 1
-                ring["in_use"] = ring["in_use"] + 1
-
-        def release(key):
-            n = owner[key]
-            left[n] = left[n] - 1
-            if left[n] == 0:
-                ring["in_use"] = ring["in_use"] - 1
-                pump()
-
-        pump()
+        w_raw = raws.tile([P, CT, C], BF16, name="w_raw")
+        src["w"] = w_raw[:]
+        for kind, b, k0, nk in pieces:
+            if kind == "w":
+                nc.sync.dma_start(
+                    out=w_raw[:, k0 : k0 + 2, :],
+                    in_=weight[0].rearrange("(ct c) o -> c ct o", c=P)[:, k0 : k0 + 2, :],
+                )
+            elif kind == "e":
+                raw = raws.tile([P, 4, 4, SIDE], BF16, name="raw_e")
+                for bb in range(B):
+                    for e in range(2):
+                        nc.sync.dma_start(out=raw[:, :, 2 * bb + e, :], in_=g_rows[bb, :, :, e * (SIDE - 1), :])
+                src["e"] = raw[:].rearrange("p t r j -> p t (r j)")
+            else:
+                raw = raws.tile([P, 4, nk * CHUNK], BF16, name="raw_%d_%d" % (b, k0))
+                nc.sync.dma_start(out=raw[:], in_=g_flat[b, :, :, k0 * CHUNK : (k0 + nk) * CHUNK])
+                for i in range(nk):
+                    src[(b, k0 + i)] = raw[:, :, i * CHUNK : (i + 1) * CHUNK]
 
         ident = const.tile([P, P], F32)
         make_identity(nc, ident[:])
@@ -212,7 +186,6 @@ def tile_gcn_layer_t_kernel(tc, x, weight, grad_out, out):
             grouped = grp.tile([P, 4 * CHUNK], BF16, align_bytes=64, tag="grouped", name="grouped_%s%d_%d" % item)
             regroup(copy, src[key], grouped[:, 0 : 4 * width])
             grouped_of[item] = grouped
-            release(key)
 
         done_q = []
 
@@ -222,7 +195,6 @@ def tile_gcn_layer_t_kernel(tc, x, weight, grad_out, out):
             regroup(nc.vector.tensor_copy, src[(b, k)][:, :, 0:v_cols], grouped[:, 0 : 4 * v_cols])
             regroup(nc.scalar.copy, src[(b, k)][:, :, v_cols:CHUNK], grouped[:, 4 * v_cols : 4 * CHUNK])
             grouped_of[item] = grouped
-            release((b, k))
 
         def stage_a_shared(item):
             kind, b, k = item
@@ -237,7 +209,6 @@ def tile_gcn_layer_t_kernel(tc, x, weight, grad_out, out):
             )
             regroup(nc.scalar.copy, src[(b, k)][:, :, G_COLS:CHUNK], grouped[:, 4 * G_COLS : 4 * CHUNK])
             grouped_of[item] = grouped
-            release((b, k))
 
         def stage_q(item):
             kind, b, k = item
@@ -387,7 +358,6 @@ def tile_gcn_layer_t_kernel(tc, x, weight, grad_out, out):
         quantise_w(0)
         stage_a_split(prep[1], 352)
         transpose_w(1)
-        release("w")
         stage_a(prep[2], nc.scalar.copy)
         stage_q(prep[1])
         quantise_w(1)

@@ -20,11 +20,9 @@ C = 512
 SIDE = 64
 HALF = SIDE // 2
 PIX = SIDE * SIDE
-CHUNK_ROWS = 8
-CHUNK = CHUNK_ROWS * SIDE
-CHUNKS = PIX // CHUNK
+SLOTS = 8
+BANK = SLOTS * SIDE
 CT = C // P
-PADDED = PIX + 2 * SIDE
 
 FLOPS = 2 * B * PIX * C * C
 BYTES = B * C * PIX * 2 + C * C * 2 + B * C * PIX * 4
@@ -32,8 +30,30 @@ BYTES = B * C * PIX * 2 + C * C * 2 + B * C * PIX * 4
 U = math.sqrt(1.5)
 NINTH = 1.0 / 9.0
 
+ROWS = ((8, 8, 8, 8, 8, 8, 8, 8), (8, 8, 8, 8, 8, 8, 8, 8))
 UNITS = ((2, 2, 2, 2), (2, 2, 1, 1, 1, 1))
-G_COLS = 128
+ORDER = (
+    ("c", 0, 0), ("c", 0, 1), ("e",), ("c", 0, 2), ("c", 0, 3), ("c", 0, 4), ("c", 0, 5), ("c", 0, 6), ("c", 0, 7),
+    ("c", 1, 0), ("c", 1, 1), ("c", 1, 2), ("c", 1, 3), ("c", 1, 4), ("c", 1, 7), ("c", 1, 5), ("c", 1, 6),
+)
+LOADS = (
+    ("c", 0, 0, 1), ("w", 0), ("w", 1), ("c", 0, 1, 1), ("c", 0, 2, 1), ("e",), ("c", 0, 3, 1),
+    ("c", 0, 4, 2), ("c", 0, 6, 2), ("c", 1, 0, 2), ("c", 1, 2, 2), ("c", 1, 4, 2), ("c", 1, 6, 2),
+)
+QUEUE = (
+    (0, 0), (0, 1), (0, 2), "e", (0, 3), (0, 4), (0, 5), (0, 6), (0, 7),
+    (1, 0), (1, 1), (1, 2), (1, 3), (1, 4), (1, 6), (1, 7), (1, 5),
+)
+FRONT = 1
+SHIFT = 1
+WARM = (8, 2)
+G_ROWS = 0
+V_ROWS = 5
+QK = 4
+RK = 5
+GB = 3
+G_EARLY = 4
+EARLY = 4
 HALVED = 2
 
 
@@ -43,307 +63,97 @@ def tile_gcn_layer_t_kernel(tc, x, weight, grad_out, out):
         ctx.enter_context(tc.manual_schedule())
         const = ctx.enter_context(tc.tile_pool(name="const", bufs=1))
         raws = ctx.enter_context(tc.tile_pool(name="raws", bufs=1))
-        grp = ctx.enter_context(tc.tile_pool(name="grp", bufs=3))
+        grp = ctx.enter_context(tc.tile_pool(name="grp", bufs=GB))
         evens = ctx.enter_context(tc.tile_pool(name="evens", bufs=8))
         small = ctx.enter_context(tc.tile_pool(name="small", bufs=4))
         eds = ctx.enter_context(tc.tile_pool(name="eds", bufs=4))
-        outs = ctx.enter_context(tc.tile_pool(name="outs", bufs=5))
+        outs = ctx.enter_context(tc.tile_pool(name="outs", bufs=4))
         psum = ctx.enter_context(tc.psum_pool(name="psum", bufs=8))
 
         g_flat = grad_out.rearrange("b (p t) i j -> b p t (i j)", t=4)
         g_rows = grad_out.rearrange("b (p t) i j -> b p t i j", t=4)
         out_v = out.rearrange("b (ct c) i j -> b c ct (i j)", c=P)
+        w_v = weight[0].rearrange("(ct c) o -> c ct o", c=P)
 
-        chunks = [("c", g // CHUNKS, g % CHUNKS) for g in range(B * CHUNKS)]
-        prep = chunks[0:2] + [("e", 0, 0)] + chunks[2:]
-        main = chunks[0:1] + [("e", 0, 0)] + chunks[1:13] + [chunks[15], chunks[13], chunks[14]]
-        n_items = len(main)
+        row0 = {}
+        rows = {}
+        piece = {}
         unit_of = {}
         for b in range(B):
-            k0 = 0
+            r = 0
+            for j, nr in enumerate(ROWS[b]):
+                row0[(b, j)] = r
+                rows[(b, j)] = nr
+                piece[(b, j)] = (r + SHIFT * (j > 0), min(r + nr + SHIFT, SIDE))
+                r += nr
+            j0 = 0
             for n in UNITS[b]:
-                for k in range(k0, k0 + n):
-                    unit_of[(b, k)] = (k0, n)
-                k0 += n
+                for j in range(j0, j0 + n):
+                    unit_of[(b, j)] = (b, j0, n)
+                j0 += n
 
-        pieces = [("c", 0, 0, 1), ("w", 0, 0, 1), ("c", 0, 1, 1), ("w", 0, 2, 1), ("e", 0, 0, 1), ("c", 0, 2, 1), ("c", 0, 3, 1)]
-        pieces += [("c", 0, k, 2) for k in (4, 6)] + [("c", 1, k, 2) for k in (0, 2, 4, 6)]
-        src = {}
+        def need(item):
+            if item[0] == "e":
+                return ["e"]
+            b, j = item[1:]
+            return [(b, i) for i in range(max(j - 1, 0), min(j + 2 - SHIFT, len(ROWS[b])))]
+
         w_raw = raws.tile([P, CT, C], BF16, name="w_raw")
-        src["w"] = w_raw[:]
-        for kind, b, k0, nk in pieces:
-            if kind == "w":
-                nc.sync.dma_start(
-                    out=w_raw[:, k0 : k0 + 2, :],
-                    in_=weight[0].rearrange("(ct c) o -> c ct o", c=P)[:, k0 : k0 + 2, :],
-                )
-            elif kind == "e":
-                raw = raws.tile([P, 4, 4, SIDE], BF16, name="raw_e")
-                for bb in range(B):
+        src = {}
+
+        def load_w(half):
+            nc.sync.dma_start(out=w_raw[:, 2 * half : 2 * half + 2, :], in_=w_v[:, 2 * half : 2 * half + 2, :])
+
+        def load(b, j, n):
+            r0 = piece[(b, j)][0]
+            r1 = piece[(b, j + n - 1)][1]
+            raw = raws.tile([P, 4, (r1 - r0) * SIDE], BF16, name="raw_%d_%d" % (b, j))
+            nc.sync.dma_start(out=raw[:], in_=g_flat[b, :, :, r0 * SIDE : r1 * SIDE])
+            for i in range(j, j + n):
+                q0, q1 = piece[(b, i)]
+                src[(b, i)] = raw[:, :, (q0 - r0) * SIDE : (q1 - r0) * SIDE]
+
+        for spec in LOADS:
+            if spec[0] == "w":
+                load_w(spec[1])
+            elif spec[0] == "e":
+                raw_e = raws.tile([P, 4, 2 * B, SIDE], BF16, name="raw_e")
+                for b in range(B):
                     for e in range(2):
-                        nc.sync.dma_start(out=raw[:, :, 2 * bb + e, :], in_=g_rows[bb, :, :, e * (SIDE - 1), :])
-                src["e"] = raw[:].rearrange("p t r j -> p t (r j)")
+                        nc.sync.dma_start(out=raw_e[:, :, 2 * b + e, :], in_=g_rows[b, :, :, e * (SIDE - 1), :])
+                src["e"] = raw_e[:].rearrange("p t r j -> p t (r j)")
             else:
-                raw = raws.tile([P, 4, nk * CHUNK], BF16, name="raw_%d_%d" % (b, k0))
-                nc.sync.dma_start(out=raw[:], in_=g_flat[b, :, :, k0 * CHUNK : (k0 + nk) * CHUNK])
-                for i in range(nk):
-                    src[(b, k0 + i)] = raw[:, :, i * CHUNK : (i + 1) * CHUNK]
+                load(*spec[1:])
 
         ident = const.tile([P, P], F32)
         make_identity(nc, ident[:])
-        codes = const.tile([P, B, PADDED], U32, align_bytes=64)
-        scales = const.tile([P, B, PADDED], U8, align_bytes=64)
-        e_codes = const.tile([P, CHUNK], U32, align_bytes=64)
-        e_scales = const.tile([P, CHUNK], U8, align_bytes=64)
+        padded = (FRONT + SIDE + 1) * SIDE
+        codes = const.tile([P, B, padded], U32, align_bytes=64)
+        scales = const.tile([P, B, padded], U8, align_bytes=64)
+        e_span = 2 * B * SIDE
+        e_codes = const.tile([P, 3 * e_span], U32, align_bytes=64)
+        e_scales = const.tile([P, 3 * e_span], U8, align_bytes=64)
         w_codes = const.tile([P, C], U32, align_bytes=64)
         w_scales = const.tile([P, C], U8, align_bytes=64)
-        extra = const.tile([P, CT, 4 * SIDE], F32)
-        nc.vector.memset(codes[:, :, 0:SIDE].bitcast(I32), 0)
-        nc.vector.memset(codes[:, :, PADDED - SIDE : PADDED].bitcast(I32), 0)
-        nc.vector.memset(scales[:, :, 0:SIDE].bitcast(I32), 0)
-        nc.vector.memset(scales[:, :, PADDED - SIDE : PADDED].bitcast(I32), 0)
-        nc.vector.memset(e_codes[:, 4 * SIDE : CHUNK].bitcast(I32), 0)
-        nc.vector.memset(e_scales[:, 4 * SIDE : CHUNK].bitcast(I32), 0)
-
-        def regroup(copy, src_ap, dst_ap):
-            copy(
-                out=dst_ap.rearrange("p (a s t) -> p a t s", s=2, t=4),
-                in_=src_ap.rearrange("p t (a s) -> p a t s", s=2)[:, :, :, ::-1],
-            )
+        nc.vector.memset(codes[:, :, 0 : FRONT * SIDE].bitcast(I32), 0)
+        nc.vector.memset(codes[:, :, padded - SIDE : padded].bitcast(I32), 0)
+        nc.vector.memset(scales[:, :, 0 : FRONT * SIDE].bitcast(I32), 0)
+        nc.vector.memset(scales[:, :, padded - SIDE : padded].bitcast(I32), 0)
+        for z in (0, 2 * e_span):
+            nc.vector.memset(e_codes[:, z : z + e_span].bitcast(I32), 0)
+            nc.vector.memset(e_scales[:, z : z + e_span].bitcast(I32), 0)
 
         grouped_w = const.tile([P, 4 * C], BF16, align_bytes=64, name="grouped_w")
-        w32 = src["w"].bitcast(F32)
+        w32 = w_raw[:].bitcast(F32)
         gw32 = grouped_w[:].bitcast(F32).rearrange("p (ct c h) -> p ct c h", ct=CT, h=2)
+
         def transpose_w(half):
-            w_t = psum.tile([P, CHUNK], F32, tag="bank", name="w_t%d" % half)
+            w_t = psum.tile([P, BANK], F32, tag="bank", name="w_t%d" % half)
             w_tv = w_t[:].rearrange("p (c2 h c) -> p c2 h c", c2=2, h=2)
             for c2 in range(2):
                 for h in range(2):
                     nc.tensor.transpose(w_tv[:, c2, h, :], w32[:, 2 * half + c2, h : C // 2 : 2], ident[:])
             nc.scalar.copy(out=gw32[:, 2 * half : 2 * half + 2, :, :], in_=w_tv.rearrange("p c2 h c -> p c2 c h"))
-
-        def multiply(bank, ct, windows):
-            for n, (rhs, rhs_scale) in enumerate(windows):
-                nc.tensor.matmul_mx(
-                    out=bank[:],
-                    lhsT=w_codes[:, ct * P : (ct + 1) * P].bitcast(E4X4),
-                    lhsT_scale=w_scales[:, ct * P : (ct + 1) * P],
-                    rhs=rhs.bitcast(E5X4),
-                    rhs_scale=rhs_scale,
-                    start=(n == 0),
-                    stop=(n == len(windows) - 1),
-                )
-
-        def column_edges(on_vector, rows, o3, ed3):
-            edge = ed3[:, :, 1:3]
-            inner = ed3[:, :, 0:4:3]
-            next_cols = o3[:, :, 1 : SIDE - 1 : SIDE - 3]
-            edge_cols = o3[:, :, 0 : SIDE : SIDE - 1]
-            if on_vector:
-                nc.vector.scalar_tensor_tensor(
-                    out=next_cols, in0=edge, scalar=(U - 1.0) / U, in1=next_cols, op0=ALU.mult, op1=ALU.add
-                )
-                nc.vector.scalar_tensor_tensor(out=edge_cols, in0=edge, scalar=U, in1=inner, op0=ALU.mult, op1=ALU.add)
-            else:
-                t1 = small.tile([P, rows, 2], F32, tag="t1")
-                t2 = small.tile([P, rows, 2], F32, tag="t2")
-                nc.gpsimd.tensor_scalar(
-                    out=t1[:], in0=edge, scalar1=(U - 1.0) / U, scalar2=0.0, op0=ALU.mult, op1=ALU.add
-                )
-                nc.gpsimd.tensor_scalar(out=t2[:], in0=edge, scalar1=U, scalar2=0.0, op0=ALU.mult, op1=ALU.add)
-                nc.gpsimd.tensor_tensor(out=next_cols, in0=next_cols, in1=t1[:], op=ALU.add)
-                nc.gpsimd.tensor_tensor(out=edge_cols, in0=t2[:], in1=inner, op=ALU.add)
-
-        extra4 = extra[:].rearrange("p ct (r j) -> p ct r j", j=SIDE)
-
-        def row_edge(o4, first, edge_row, which, ct0=0, nct=CT):
-            two = o4[:, :, first : first + 2, :]
-            nc.gpsimd.tensor_tensor(
-                out=two,
-                in0=two,
-                in1=extra4[:, ct0 : ct0 + nct, which, :].unsqueeze(2).to_broadcast([P, nct, 2, SIDE]),
-                op=ALU.add,
-            )
-            nc.gpsimd.tensor_scalar(
-                out=o4[:, :, edge_row, :], in0=o4[:, :, edge_row, :], scalar1=U, scalar2=0.0, op0=ALU.mult, op1=ALU.add
-            )
-
-        grouped_of = {}
-        work = {}
-        unit_tiles = {}
-
-        def geometry(item):
-            kind, b, k = item
-            if kind == "e":
-                return 4 * SIDE, (U - 1.0) * NINTH, 0, 0, 1
-            k0, n = unit_of[(b, k)]
-            return CHUNK, NINTH, (k - k0), k0, n
-
-        def stage_a(item, copy):
-            kind, b, k = item
-            key = "e" if kind == "e" else (b, k)
-            width = geometry(item)[0]
-            grouped = grp.tile([P, 4 * CHUNK], BF16, align_bytes=64, tag="grouped", name="grouped_%s%d_%d" % item)
-            regroup(copy, src[key], grouped[:, 0 : 4 * width])
-            grouped_of[item] = grouped
-
-        done_q = []
-
-        def stage_a_split(item, v_cols):
-            kind, b, k = item
-            grouped = grp.tile([P, 4 * CHUNK], BF16, align_bytes=64, tag="grouped", name="grouped_%s%d_%d" % item)
-            regroup(nc.vector.tensor_copy, src[(b, k)][:, :, 0:v_cols], grouped[:, 0 : 4 * v_cols])
-            regroup(nc.scalar.copy, src[(b, k)][:, :, v_cols:CHUNK], grouped[:, 4 * v_cols : 4 * CHUNK])
-            grouped_of[item] = grouped
-
-        def stage_a_shared(item):
-            kind, b, k = item
-            grouped = grp.tile([P, 4 * CHUNK], BF16, align_bytes=64, tag="grouped", name="grouped_%s%d_%d" % item)
-            nc.gpsimd.tensor_scalar(
-                out=grouped[:, 0 : 4 * G_COLS].rearrange("p (a s t) -> p a s t", s=2, t=4),
-                in0=src[(b, k)][:, :, 0:G_COLS].rearrange("p t (a s) -> p a s t", s=2)[:, :, ::-1, :],
-                scalar1=1.0,
-                scalar2=0.0,
-                op0=ALU.mult,
-                op1=ALU.add,
-            )
-            regroup(nc.scalar.copy, src[(b, k)][:, :, G_COLS:CHUNK], grouped[:, 4 * G_COLS : 4 * CHUNK])
-            grouped_of[item] = grouped
-
-        def stage_q(item):
-            kind, b, k = item
-            done_q.append(item)
-            grouped = grouped_of[item]
-            if kind == "e":
-                nc.vector.quantize_mx(
-                    out=e_codes[:, 0 : 4 * SIDE].bitcast(E5X4),
-                    scales=e_scales[:, 0 : 4 * SIDE],
-                    in_=grouped[:, 0 : 16 * SIDE],
-                )
-            else:
-                c0 = SIDE + k * CHUNK
-                nc.vector.quantize_mx(
-                    out=codes[:, b, c0 : c0 + CHUNK].bitcast(E5X4), scales=scales[:, b, c0 : c0 + CHUNK], in_=grouped[:]
-                )
-
-        def stage_m(item, ct):
-            kind, b, k = item
-            bank = psum.tile([P, CHUNK], F32, tag="bank", name="bank_%s%d_%d_%d" % (kind, b, k, ct))
-            assert item in done_q
-            assert kind == "e" or k == 0 or ("c", b, k - 1) in done_q
-            assert kind == "e" or k == CHUNKS - 1 or ("c", b, k + 1) in done_q
-            if kind == "e":
-                multiply(bank, ct, [(e_codes[:], e_scales[:])])
-            else:
-                windows = []
-                for d in (-1, 0, 1):
-                    c0 = SIDE + k * CHUNK + d * SIDE
-                    windows.append((codes[:, b, c0 : c0 + CHUNK], scales[:, b, c0 : c0 + CHUNK]))
-                multiply(bank, ct, windows)
-            work[(item, ct)] = [bank, None, None]
-
-        def stage_e(item, ct):
-            kind, b, k = item
-            width, c, part, k0, n = geometry(item)
-            ukey = (kind, b, k0)
-            if part == 0 and ct == 0:
-                ed_new = eds.tile([P, CT, n * width // SIDE, 4], F32, tag="ed", name="ed_%s%d_%d" % item)
-                unit_tiles[ukey] = [ed_new, None]
-            ed = unit_tiles[ukey][0]
-            rows = width // SIDE
-            xv = work[(item, ct)][0][:, 0:width]
-            nc.scalar.activation(
-                out=ed[:, ct, part * rows : (part + 1) * rows, :].rearrange("p r (s k) -> p r s k", k=2),
-                in_=xv.rearrange("p (r s k) -> p r s k", s=HALF, k=2)[:, :, 0 : HALF : HALF - 1, :],
-                func=ACT.Copy,
-                scale=U * c,
-            )
-            even = evens.tile([P, CHUNK // 2], F32, tag="even", name="even_%s%d_%d_%d" % (kind, b, k, ct))
-            nc.scalar.activation(out=even[:, 0 : width // 2], in_=xv[:, 1:width:2], func=ACT.Copy, scale=c)
-            work[(item, ct)][1] = even
-
-        def stage_p(item, ct):
-            width, c, part, k0, n = geometry(item)
-            bank, even, unused = work[(item, ct)]
-            m = width // 2 - 1
-            pair = small.tile([P, CHUNK // 2], F32, tag="pair", name="pair_%s%d_%d_%d" % (item[0], item[1], item[2], ct))
-            nc.vector.scalar_tensor_tensor(
-                out=pair[:, 0:m],
-                in0=bank[:, 0 : width - 2 : 2],
-                scalar=c,
-                in1=even[:, 1 : width // 2],
-                op0=ALU.mult,
-                op1=ALU.add,
-            )
-            work[(item, ct)][2] = pair
-
-        def out_tile(item):
-            kind, b, k = item
-            width, c, part, k0, n = geometry(item)
-            if kind == "e":
-                return extra
-            ukey = (kind, b, k0)
-            if unit_tiles[ukey][1] is None:
-                unit_tiles[ukey][1] = outs.tile([P, CT, n * CHUNK], F32, tag="o", name="o_%d_%d" % (b, k0))
-            return unit_tiles[ukey][1]
-
-        def stage_h(item, ct):
-            width, c, part, k0, n = geometry(item)
-            bank, even, pair = work[(item, ct)]
-            m = width // 2 - 1
-            o_flat = out_tile(item)[:, ct, part * width : (part + 1) * width]
-            nc.vector.scalar_tensor_tensor(
-                out=o_flat[:, 1 : width - 1].rearrange("p (m e) -> p m e", e=2),
-                in0=bank[:, 1 : width - 1].rearrange("p (m e) -> p m e", e=2),
-                scalar=c,
-                in1=pair[:, 0:m].unsqueeze(2).to_broadcast([P, m, 2]),
-                op0=ALU.mult,
-                op1=ALU.add,
-            )
-
-        def finish_unit(item):
-            kind, b, k = item
-            width, c, part, k0, n = geometry(item)
-            if part != n - 1:
-                return
-            o_t = out_tile(item)
-            ed = unit_tiles[(kind, b, k0)][0]
-            rows = n * width // SIDE
-            column_edges(
-                False,
-                CT * rows,
-                o_t[:].rearrange("p ct (r j) -> p (ct r) j", j=SIDE),
-                ed[:].rearrange("p ct r k -> p (ct r) k"),
-            )
-            if kind == "e":
-                return
-            o4 = o_t[:].rearrange("p ct (r j) -> p ct r j", j=SIDE)
-            if k0 == 0:
-                row_edge(o4, 0, 0, 2 * b)
-            if k == CHUNKS - 1:
-                row_edge(o4, rows - 2, rows - 1, 2 * b + 1)
-            nc.sync.dma_start(out=out_v[b, :, :, k0 * CHUNK : (k0 + n) * CHUNK], in_=o_t[:])
-
-        def finish_half(item, ct0):
-            kind, b, k = item
-            o_t = out_tile(item)[:, ct0 : ct0 + 2, :]
-            ed = unit_tiles[(kind, b, k)][0][:, ct0 : ct0 + 2, :, :]
-            column_edges(
-                False,
-                2 * CHUNK_ROWS,
-                o_t.rearrange("p ct (r j) -> p (ct r) j", j=SIDE),
-                ed.rearrange("p ct r k -> p (ct r) k"),
-            )
-            if k == CHUNKS - 1:
-                row_edge(o_t.rearrange("p ct (r j) -> p ct r j", j=SIDE), CHUNK_ROWS - 2, CHUNK_ROWS - 1, 2 * b + 1, ct0, 2)
-            nc.sync.dma_start(out=out_v[b, :, ct0 : ct0 + 2, k * CHUNK : (k + 1) * CHUNK], in_=o_t)
-
-        def finish_last(item, ct):
-            kind, b, k = item
-            o_t = out_tile(item)
-            ed = unit_tiles[(kind, b, k)][0]
-            column_edges(True, CHUNK_ROWS, o_t[:, ct, :].rearrange("p (r j) -> p r j", j=SIDE), ed[:, ct, :, :])
-            nc.sync.dma_start(out=out_v[b, :, ct, k * CHUNK : (k + 1) * CHUNK], in_=o_t[:, ct, :])
 
         def quantise_w(half):
             nc.vector.quantize_mx(
@@ -352,47 +162,337 @@ def tile_gcn_layer_t_kernel(tc, x, weight, grad_out, out):
                 in_=grouped_w[:, half * 2 * C : (half + 1) * 2 * C],
             )
 
-        stage_a_split(prep[0], 352)
+        dummy = const.tile([P, BANK], BF16)
+        nc.vector.memset(dummy[:], 0.0)
+
+        def warm_up(count):
+            for n in range(count):
+                bank = psum.tile([P, BANK], F32, tag="bank", name="dummy_%d_%d" % (count, n))
+                nc.tensor.matmul(out=bank[:], lhsT=dummy[:, 0:P], rhs=dummy[:], start=True, stop=True)
+
+        grouped_of = {}
+
+        def move_on_gpsimd(out, in_):
+            nc.gpsimd.tensor_scalar(out=out, in0=in_, scalar1=1.0, scalar2=0.0, op0=ALU.mult, op1=ALU.add)
+
+        def regroup(bj, shares):
+            n = 2 * B if bj == "e" else piece[bj][1] - piece[bj][0]
+            grouped = grp.tile(
+                [P, 4 * (SLOTS + 1) * SIDE], BF16, align_bytes=64, tag="grouped", name="grouped_%s_%s" % (bj[0], bj[-1])
+            )
+            grouped_of[bj] = grouped
+            r = 0
+            for copy, nr in shares:
+                nr = min(nr, n - r)
+                if nr == 0:
+                    continue
+                s = src[bj][:, :, r * SIDE : (r + nr) * SIDE]
+                d = grouped[:, r * 4 * SIDE : (r + nr) * 4 * SIDE]
+                if copy == "gpsimd":
+                    move_on_gpsimd(
+                        d.rearrange("p (a s t) -> p a s t", s=2, t=4),
+                        s.rearrange("p t (a s) -> p a s t", s=2)[:, :, ::-1, :],
+                    )
+                else:
+                    (nc.vector.tensor_copy if copy == "vector" else nc.scalar.copy)(
+                        out=d.rearrange("p (a s t) -> p a t s", s=2, t=4),
+                        in_=s.rearrange("p t (a s) -> p a t s", s=2)[:, :, :, ::-1],
+                    )
+                r += nr
+
+        done = []
+
+        def quantise(bj):
+            if bj in done:
+                return
+            done.append(bj)
+            grouped = grouped_of[bj]
+            if bj == "e":
+                nc.vector.quantize_mx(
+                    out=e_codes[:, e_span : 2 * e_span].bitcast(E5X4),
+                    scales=e_scales[:, e_span : 2 * e_span],
+                    in_=grouped[:, 0 : 4 * e_span],
+                )
+                return
+            b = bj[0]
+            r, r1 = piece[bj]
+            at = 0
+            for n in (8, 4, 2, 1):
+                if r + n <= r1:
+                    c0 = (FRONT + r) * SIDE
+                    nc.vector.quantize_mx(
+                        out=codes[:, b, c0 : c0 + n * SIDE].bitcast(E5X4),
+                        scales=scales[:, b, c0 : c0 + n * SIDE],
+                        in_=grouped[:, at * 4 * SIDE : (at + n) * 4 * SIDE],
+                    )
+                    r += n
+                    at += n
+
+        work = {}
+
+        def banks_of(item):
+            return 2 if item[0] == "e" else CT
+
+        def width_of(item):
+            return BANK if item[0] == "e" else rows[item[1:]] * SIDE
+
+        def factor_of(item):
+            return (U - 1.0) * NINTH if item[0] == "e" else NINTH
+
+        def name_of(item):
+            return "_".join([str(v) for v in item])
+
+        def stage_m(item, ct):
+            for bj in need(item):
+                assert bj in done
+            bank = psum.tile([P, BANK], F32, tag="bank", name="bank_%s_%d" % (name_of(item), ct))
+            windows = []
+            if item[0] == "e":
+                off = 0
+                for n, c0 in enumerate((e_span, 0)):
+                    windows.append((2 * ct + n, e_codes[:, c0 : c0 + BANK], e_scales[:, c0 : c0 + BANK]))
+            else:
+                b, j = item[1:]
+                off = BANK - rows[(b, j)] * SIDE
+                for d in (-1, 0, 1):
+                    c0 = (FRONT + row0[(b, j)] + d) * SIDE - off
+                    windows.append((ct, codes[:, b, c0 : c0 + BANK], scales[:, b, c0 : c0 + BANK]))
+            for n, (wt, rhs, rhs_scale) in enumerate(windows):
+                nc.tensor.matmul_mx(
+                    out=bank[:],
+                    lhsT=w_codes[:, wt * P : (wt + 1) * P].bitcast(E4X4),
+                    lhsT_scale=w_scales[:, wt * P : (wt + 1) * P],
+                    rhs=rhs.bitcast(E5X4),
+                    rhs_scale=rhs_scale,
+                    start=(n == 0),
+                    stop=(n == len(windows) - 1),
+                )
+            work[(item, ct)] = {"x": bank[:, off : off + width_of(item)]}
+
+        out_of = {}
+        ed_of = {}
+
+        def group_of(item):
+            if item[0] == "e":
+                return item, 0, width_of(item) // SIDE
+            b, j0, n = unit_of[item[1:]]
+            return (b, j0), row0[item[1:]] - row0[(b, j0)], sum(ROWS[b][j0 : j0 + n])
+
+        def out_rows(item, ct):
+            key, at, total = group_of(item)
+            if key not in out_of:
+                if item[0] == "e":
+                    o_new = raws.tile([P, 2, total * SIDE], F32, name="extra")
+                else:
+                    o_new = outs.tile([P, CT, total * SIDE], F32, tag="o", name="o_" + name_of(item))
+                out_of[key] = o_new
+            return out_of[key][:, ct, at * SIDE : at * SIDE + width_of(item)]
+
+        def stage_e(item, ct):
+            key, at, total = group_of(item)
+            if key not in ed_of:
+                ed_new = eds.tile([P, banks_of(item), total, 4], F32, tag="ed", name="ed_" + name_of(item))
+                ed_of[key] = ed_new
+            width = width_of(item)
+            n = width // SIDE
+            xv = work[(item, ct)]["x"]
+            nc.scalar.activation(
+                out=ed_of[key][:, ct, at : at + n, :].rearrange("p r (s k) -> p r s k", k=2),
+                in_=xv.rearrange("p (r s k) -> p r s k", s=HALF, k=2)[:, :, 0 : HALF : HALF - 1, :],
+                func=ACT.Copy,
+                scale=(U if item == ORDER[-1] else U - 1.0) * factor_of(item),
+            )
+            even = evens.tile([P, BANK // 2], F32, tag="even", name="even_%s_%d" % (name_of(item), ct))
+            nc.scalar.activation(out=even[:, 0 : width // 2], in_=xv[:, 1:width:2], func=ACT.Copy, scale=factor_of(item))
+            work[(item, ct)]["even"] = even
+
+        def stage_p(item, ct):
+            width = width_of(item)
+            m = width // 2 - 1
+            pair = small.tile([P, BANK // 2], F32, tag="pair", name="pair_%s_%d" % (name_of(item), ct))
+            nc.vector.scalar_tensor_tensor(
+                out=pair[:, 0:m],
+                in0=work[(item, ct)]["x"][:, 0 : width - 2 : 2],
+                scalar=factor_of(item),
+                in1=work[(item, ct)]["even"][:, 1 : width // 2],
+                op0=ALU.mult,
+                op1=ALU.add,
+            )
+            work[(item, ct)]["pair"] = pair
+
+        def stage_h(item, ct):
+            width = width_of(item)
+            m = width // 2 - 1
+            nc.vector.scalar_tensor_tensor(
+                out=out_rows(item, ct)[:, 1 : width - 1].rearrange("p (m e) -> p m e", e=2),
+                in0=work[(item, ct)]["x"][:, 1 : width - 1].rearrange("p (m e) -> p m e", e=2),
+                scalar=factor_of(item),
+                in1=work[(item, ct)]["pair"][:, 0:m].unsqueeze(2).to_broadcast([P, m, 2]),
+                op0=ALU.mult,
+                op1=ALU.add,
+            )
+
+        sums_of = {}
+
+        def edge_view(key, ct0, nct):
+            return ed_of[key][:, ct0 : ct0 + nct, :, :].rearrange("p ct r k -> p (ct r) k")
+
+        def prepare(key, ct0, nct):
+            ed3 = edge_view(key, ct0, nct)
+            sums = small.tile([P, ed3.shape[1], 2], F32, tag="sums", name="sums")
+            nc.vector.scalar_tensor_tensor(
+                out=sums[:], in0=ed3[:, :, 1:3], scalar=U, in1=ed3[:, :, 0:4:3], op0=ALU.mult, op1=ALU.add
+            )
+            sums_of[(key, ct0)] = sums
+
+        def fix_columns(on_vector, key, ct0, nct):
+            o3 = out_of[key][:, ct0 : ct0 + nct, :].rearrange("p ct (r j) -> p (ct r) j", j=SIDE)
+            ed3 = edge_view(key, ct0, nct)
+            edge = ed3[:, :, 1:3]
+            next_cols = o3[:, :, 1 : SIDE - 1 : SIDE - 3]
+            edge_cols = o3[:, :, 0 : SIDE : SIDE - 1]
+            if on_vector:
+                nc.vector.scalar_tensor_tensor(
+                    out=next_cols, in0=edge, scalar=(U - 1.0) / U, in1=next_cols, op0=ALU.mult, op1=ALU.add
+                )
+                nc.vector.scalar_tensor_tensor(
+                    out=edge_cols, in0=edge, scalar=U, in1=ed3[:, :, 0:4:3], op0=ALU.mult, op1=ALU.add
+                )
+            else:
+                nc.gpsimd.tensor_scalar(
+                    out=edge_cols,
+                    in0=sums_of[(key, ct0)][:],
+                    scalar1=U / (U - 1.0),
+                    scalar2=0.0,
+                    op0=ALU.mult,
+                    op1=ALU.add,
+                )
+                nc.gpsimd.tensor_tensor(out=next_cols, in0=next_cols, in1=edge, op=ALU.add)
+
+        def border_rows(key, ct0, nct):
+            b, j0 = key
+            n = unit_of[key][2]
+            first = row0[key]
+            last = first + sum(ROWS[b][j0 : j0 + n]) - 1
+            o4 = out_of[key][:, ct0 : ct0 + nct, :].rearrange("p ct (r j) -> p ct r j", j=SIDE)
+            for row, r0 in ((0, 0), (SIDE - 1, last - first - 1)):
+                if not first <= row <= last:
+                    continue
+                at = 0 if row == 0 else last - first
+                ex4 = out_of[("e",)][:].rearrange("p h (ct r j) -> p (h ct) r j", ct=2, j=SIDE)
+                i = 2 * b + (row > 0)
+                two = o4[:, :, r0 : r0 + 2, :]
+                nc.gpsimd.tensor_tensor(
+                    out=two,
+                    in0=two,
+                    in1=ex4[:, ct0 : ct0 + nct, i, :].unsqueeze(2).to_broadcast([P, nct, 2, SIDE]),
+                    op=ALU.add,
+                )
+                nc.gpsimd.tensor_scalar(
+                    out=o4[:, :, at, :], in0=o4[:, :, at, :], scalar1=U, scalar2=0.0, op0=ALU.mult, op1=ALU.add
+                )
+
+        def store(key, ct0, nct):
+            b, j0 = key
+            r0 = row0[key]
+            r1 = r0 + sum(ROWS[b][j0 : j0 + unit_of[key][2]])
+            nc.sync.dma_start(
+                out=out_v[b, :, ct0 : ct0 + nct, r0 * SIDE : r1 * SIDE], in_=out_of[key][:, ct0 : ct0 + nct, :]
+            )
+
+        waiting = []
+
+        def ready(key):
+            b, j0 = key
+            inside = j0 > 0 and j0 + unit_of[key][2] < len(ROWS[b])
+            return inside or ("e",) in finished
+
+        finished = []
+
+        def finish(item):
+            finished.append(item)
+            if item[0] == "e":
+                fix_columns(False, item, 0, 2)
+            else:
+                b, j0, n = unit_of[item[1:]]
+                if item[2] != j0 + n - 1:
+                    return
+                fix_columns(False, (b, j0), 0, CT)
+                waiting.append((b, j0))
+            for key in list(waiting):
+                if ready(key):
+                    waiting.remove(key)
+                    border_rows(key, 0, CT)
+                    store(key, 0, CT)
+
+        def finish_part(item, ct0, nct, on_vector):
+            key = item[1:]
+            assert unit_of[key][1:] == (key[1], 1) and ready(key)
+            fix_columns(on_vector, key, ct0, nct)
+            border_rows(key, ct0, nct)
+            store(key, ct0, nct)
+
+        n_items = len(ORDER)
+        place = {"regroup": 0, "quantise": 0}
+
+        def advance(kind, call, count):
+            while place[kind] < min(count, len(QUEUE)):
+                call(QUEUE[place[kind]])
+                place[kind] += 1
+
+        def regroup_next(bj):
+            if bj == "e":
+                regroup(bj, (("gpsimd", 2 * B),))
+            elif bj in QUEUE[0:2]:
+                regroup(bj, (("vector", V_ROWS), ("scalar", SLOTS + 1)))
+            elif bj in QUEUE[2:EARLY]:
+                regroup(bj, (("gpsimd", G_EARLY), ("scalar", SLOTS + 1)))
+            else:
+                regroup(bj, (("gpsimd", G_ROWS), ("scalar", SLOTS + 1)))
+
+        advance("regroup", regroup_next, 1)
+        warm_up(WARM[0])
         transpose_w(0)
-        stage_q(prep[0])
-        quantise_w(0)
-        stage_a_split(prep[1], 352)
         transpose_w(1)
-        stage_a(prep[2], nc.scalar.copy)
-        stage_q(prep[1])
+        warm_up(WARM[1])
+        advance("quantise", quantise, 1)
+        quantise_w(0)
+        advance("regroup", regroup_next, 2)
         quantise_w(1)
-        stage_q(prep[2])
-        stage_a_split(prep[3], 352)
+        advance("quantise", quantise, 2)
         for i in range(-1, n_items):
-            if i + 1 < n_items:
-                for ct in range(CT):
-                    stage_m(main[i + 1], ct)
-                    stage_e(main[i + 1], ct)
-            if i + 5 < n_items:
-                stage_a_shared(prep[i + 5])
+            item = ORDER[i] if i >= 0 else None
+            follower = ORDER[i + 1] if i + 1 < n_items else None
+            if follower:
+                for ct in range(banks_of(follower)):
+                    stage_m(follower, ct)
+                    stage_e(follower, ct)
+            advance("regroup", regroup_next, i + RK)
             last = i == n_items - 1
             halves = n_items - 1 - HALVED <= i < n_items - 1
-            banks = []
-            if i >= 0:
-                banks = list(range(CT))
-            for n in range(len(banks) + 1):
-                if n + 1 < len(banks):
-                    stage_p(main[i], banks[n + 1])
-                if n + 1 == max(len(banks), 1):
-                    if i >= 0 and i + 3 < n_items - 1:
-                        stage_q(prep[i + 3])
-                    if i + 3 == n_items - 2:
-                        stage_q(prep[i + 4])
-                    if i + 1 < n_items:
-                        stage_p(main[i + 1], 0)
-                if n < len(banks):
-                    stage_h(main[i], banks[n])
-                    if last and n > 0:
-                        finish_last(main[i], banks[n - 1])
+            n_banks = banks_of(item) if item else 0
+            for n in range(max(n_banks, 1)):
+                if n + 1 < n_banks:
+                    stage_p(item, n + 1)
+                else:
+                    if item:
+                        advance("quantise", quantise, i + QK)
+                    if follower:
+                        stage_p(follower, 0)
+                if n < n_banks:
                     if halves and n % 2 == 1:
-                        finish_half(main[i], n - 1)
-            if i >= 0:
+                        prepare(item[1:], n - 1, 2)
+                    if n == n_banks - 1 and not halves and not last:
+                        key, at, total = group_of(item)
+                        if at + width_of(item) // SIDE == total:
+                            prepare(key, 0, n_banks)
+                    stage_h(item, n)
+                    if last and n > 0:
+                        finish_part(item, n - 1, 1, True)
+                    if halves and n % 2 == 1:
+                        finish_part(item, n - 1, 2, False)
+            if item:
                 if last:
-                    finish_last(main[i], CT - 1)
+                    finish_part(item, CT - 1, 1, True)
                 elif not halves:
-                    finish_unit(main[i])
+                    finish(item)

@@ -52,8 +52,8 @@ V_ROWS = 5
 QK = 4
 RK = 5
 GB = 3
-G_EARLY = 4
-EARLY = 4
+G_EARLY = 3
+EARLY = 6
 HALVED = 2
 
 
@@ -300,7 +300,7 @@ def tile_gcn_layer_t_kernel(tc, x, weight, grad_out, out):
                 out=ed_of[key][:, ct, at : at + n, :].rearrange("p r (s k) -> p r s k", k=2),
                 in_=xv.rearrange("p (r s k) -> p r s k", s=HALF, k=2)[:, :, 0 : HALF : HALF - 1, :],
                 func=ACT.Copy,
-                scale=(U if item == ORDER[-1] else U - 1.0) * factor_of(item),
+                scale=U * factor_of(item),
             )
             even = evens.tile([P, BANK // 2], F32, tag="even", name="even_%s_%d" % (name_of(item), ct))
             nc.scalar.activation(out=even[:, 0 : width // 2], in_=xv[:, 1:width:2], func=ACT.Copy, scale=factor_of(item))
@@ -332,42 +332,33 @@ def tile_gcn_layer_t_kernel(tc, x, weight, grad_out, out):
                 op1=ALU.add,
             )
 
-        sums_of = {}
-
-        def edge_view(key, ct0, nct):
-            return ed_of[key][:, ct0 : ct0 + nct, :, :].rearrange("p ct r k -> p (ct r) k")
-
-        def prepare(key, ct0, nct):
-            ed3 = edge_view(key, ct0, nct)
-            sums = small.tile([P, ed3.shape[1], 2], F32, tag="sums", name="sums")
-            nc.vector.scalar_tensor_tensor(
-                out=sums[:], in0=ed3[:, :, 1:3], scalar=U, in1=ed3[:, :, 0:4:3], op0=ALU.mult, op1=ALU.add
-            )
-            sums_of[(key, ct0)] = sums
-
-        def fix_columns(on_vector, key, ct0, nct):
-            o3 = out_of[key][:, ct0 : ct0 + nct, :].rearrange("p ct (r j) -> p (ct r) j", j=SIDE)
-            ed3 = edge_view(key, ct0, nct)
+        def column_edges(on_vector, n, o3, ed3):
             edge = ed3[:, :, 1:3]
+            inner = ed3[:, :, 0:4:3]
             next_cols = o3[:, :, 1 : SIDE - 1 : SIDE - 3]
             edge_cols = o3[:, :, 0 : SIDE : SIDE - 1]
             if on_vector:
                 nc.vector.scalar_tensor_tensor(
                     out=next_cols, in0=edge, scalar=(U - 1.0) / U, in1=next_cols, op0=ALU.mult, op1=ALU.add
                 )
-                nc.vector.scalar_tensor_tensor(
-                    out=edge_cols, in0=edge, scalar=U, in1=ed3[:, :, 0:4:3], op0=ALU.mult, op1=ALU.add
-                )
+                nc.vector.scalar_tensor_tensor(out=edge_cols, in0=edge, scalar=U, in1=inner, op0=ALU.mult, op1=ALU.add)
             else:
-                nc.gpsimd.tensor_scalar(
-                    out=edge_cols,
-                    in0=sums_of[(key, ct0)][:],
-                    scalar1=U / (U - 1.0),
-                    scalar2=0.0,
-                    op0=ALU.mult,
-                    op1=ALU.add,
-                )
-                nc.gpsimd.tensor_tensor(out=next_cols, in0=next_cols, in1=edge, op=ALU.add)
+                t1 = small.tile([P, n, 2], F32, tag="t1", name="t1")
+                t2 = small.tile([P, n, 2], F32, tag="t2", name="t2")
+                nc.gpsimd.tensor_scalar(out=t1[:], in0=edge, scalar1=(U - 1.0) / U, scalar2=0.0, op0=ALU.mult, op1=ALU.add)
+                nc.gpsimd.tensor_scalar(out=t2[:], in0=edge, scalar1=U, scalar2=0.0, op0=ALU.mult, op1=ALU.add)
+                nc.gpsimd.tensor_tensor(out=next_cols, in0=next_cols, in1=t1[:], op=ALU.add)
+                nc.gpsimd.tensor_tensor(out=edge_cols, in0=t2[:], in1=inner, op=ALU.add)
+
+        def fix_columns(on_vector, key, ct0, nct):
+            o = out_of[key][:, ct0 : ct0 + nct, :]
+            n = nct * o.shape[2] // SIDE
+            column_edges(
+                on_vector,
+                n,
+                o.rearrange("p ct (r j) -> p (ct r) j", j=SIDE),
+                ed_of[key][:, ct0 : ct0 + nct, :, :].rearrange("p ct r k -> p (ct r) k"),
+            )
 
         def border_rows(key, ct0, nct):
             b, j0 = key
@@ -480,12 +471,6 @@ def tile_gcn_layer_t_kernel(tc, x, weight, grad_out, out):
                     if follower:
                         stage_p(follower, 0)
                 if n < n_banks:
-                    if halves and n % 2 == 1:
-                        prepare(item[1:], n - 1, 2)
-                    if n == n_banks - 1 and not halves and not last:
-                        key, at, total = group_of(item)
-                        if at + width_of(item) // SIDE == total:
-                            prepare(key, 0, n_banks)
                     stage_h(item, n)
                     if last and n > 0:
                         finish_part(item, n - 1, 1, True)

@@ -31,10 +31,10 @@ U = math.sqrt(1.5)
 NINTH = 1.0 / 9.0
 
 ROWS = ((8, 8, 8, 8, 8, 8, 8, 8), (8, 8, 8, 8, 8, 8, 8, 8))
-UNITS = ((2, 2, 2, 2), (2, 2, 1, 1, 1, 1))
+UNITS = ((2, 2, 2, 2), (2, 1, 1, 1, 1, 1, 1))
 ORDER = (
     ("c", 0, 0), ("c", 0, 1), ("e",), ("c", 0, 2), ("c", 0, 3), ("c", 0, 4), ("c", 0, 5), ("c", 0, 6), ("c", 0, 7),
-    ("c", 1, 0), ("c", 1, 1), ("c", 1, 2), ("c", 1, 3), ("c", 1, 4), ("c", 1, 7), ("c", 1, 5), ("c", 1, 6),
+    ("c", 1, 0), ("c", 1, 1), ("c", 1, 2), ("c", 1, 7), ("c", 1, 3), ("c", 1, 4), ("c", 1, 5), ("c", 1, 6),
 )
 LOADS = (
     ("c", 0, 0, 1), ("w", 0), ("w", 1), ("c", 0, 1, 1), ("c", 0, 2, 1), ("e",), ("c", 0, 3, 1),
@@ -42,19 +42,20 @@ LOADS = (
 )
 QUEUE = (
     (0, 0), (0, 1), (0, 2), "e", (0, 3), (0, 4), (0, 5), (0, 6), (0, 7),
-    (1, 0), (1, 1), (1, 2), (1, 3), (1, 4), (1, 6), (1, 7), (1, 5),
+    (1, 0), (1, 1), (1, 2), (1, 6), (1, 7), (1, 3), (1, 4), (1, 5),
 )
 FRONT = 1
 SHIFT = 1
 WARM = (8, 2)
-G_ROWS = 0
-V_ROWS = 5
+V_P0 = 6
+V_P1 = 5
 QK = 4
 RK = 5
 GB = 3
-G_EARLY = 3
-EARLY = 6
+G_SHARE = (0, 0, 5, 4, 3, 3)
+EAGER_ITEMS = (0,)
 HALVED = 2
+LAST_G = 2
 
 
 def tile_gcn_layer_t_kernel(tc, x, weight, grad_out, out):
@@ -435,11 +436,10 @@ def tile_gcn_layer_t_kernel(tc, x, weight, grad_out, out):
             if bj == "e":
                 regroup(bj, (("gpsimd", 2 * B),))
             elif bj in QUEUE[0:2]:
-                regroup(bj, (("vector", V_ROWS), ("scalar", SLOTS + 1)))
-            elif bj in QUEUE[2:EARLY]:
-                regroup(bj, (("gpsimd", G_EARLY), ("scalar", SLOTS + 1)))
+                regroup(bj, (("vector", V_P0 if bj == QUEUE[0] else V_P1), ("scalar", SLOTS + 1)))
             else:
-                regroup(bj, (("gpsimd", G_ROWS), ("scalar", SLOTS + 1)))
+                n = QUEUE.index(bj)
+                regroup(bj, (("gpsimd", G_SHARE[n] if n < len(G_SHARE) else 0), ("scalar", SLOTS + 1)))
 
         advance("regroup", regroup_next, 1)
         warm_up(WARM[0])
@@ -462,8 +462,24 @@ def tile_gcn_layer_t_kernel(tc, x, weight, grad_out, out):
             last = i == n_items - 1
             halves = n_items - 1 - HALVED <= i < n_items - 1
             n_banks = banks_of(item) if item else 0
+            if last:
+                for n in range(CT):
+                    if n < 2:
+                        stage_p(item, n + 1)
+                    stage_h(item, n)
+                    if n == 2:
+                        stage_p(item, 3)
+                    finish_part(item, n, 1, n >= LAST_G)
+                break
+            eager = i in EAGER_ITEMS
             for n in range(max(n_banks, 1)):
-                if n + 1 < n_banks:
+                if eager:
+                    if n > 0:
+                        stage_p(item, n)
+                    if n == n_banks - 1:
+                        advance("quantise", quantise, i + QK)
+                        stage_p(follower, 0)
+                elif n + 1 < n_banks:
                     stage_p(item, n + 1)
                 else:
                     if item:
@@ -472,12 +488,7 @@ def tile_gcn_layer_t_kernel(tc, x, weight, grad_out, out):
                         stage_p(follower, 0)
                 if n < n_banks:
                     stage_h(item, n)
-                    if last and n > 0:
-                        finish_part(item, n - 1, 1, True)
                     if halves and n % 2 == 1:
                         finish_part(item, n - 1, 2, False)
-            if item:
-                if last:
-                    finish_part(item, CT - 1, 1, True)
-                elif not halves:
-                    finish(item)
+            if item and not halves:
+                finish(item)

@@ -55,7 +55,7 @@ GB = 3
 G_SHARE = (0, 0, 5, 4, 3, 3)
 EAGER_ITEMS = (0,)
 HALVED = 2
-LAST_G = 2
+LAST_G = 1
 
 
 def tile_gcn_layer_t_kernel(tc, x, weight, grad_out, out):

from contextlib import ExitStack
import math

import concourse.mybir as mybir
from concourse.masks import make_identity

F32 = mybir.dt.float32
BF16 = mybir.dt.bfloat16
U32 = mybir.dt.uint32
U8 = mybir.dt.uint8
I32 = mybir.dt.int32
E4X4 = mybir.dt.float8_e4m3fn_x4
E5X4 = mybir.dt.float8_e5m2_x4
ALU = mybir.AluOpType
ACT = mybir.ActivationFunctionType

P = 128
B = 2
C = 512
SIDE = 64
HALF = SIDE // 2
PIX = SIDE * SIDE
SLOTS = 8
BANK = SLOTS * SIDE
CT = C // P

FLOPS = 2 * B * PIX * C * C
BYTES = B * C * PIX * 2 + C * C * 2 + B * C * PIX * 4

U = math.sqrt(1.5)
NINTH = 1.0 / 9.0

ROWS = ((8, 8, 8, 8, 8, 8, 8, 8), (8, 8, 8, 8, 8, 8, 8, 8))
UNITS = ((2, 2, 2, 2), (2, 1, 1, 1, 1, 1, 1))
ORDER = (
    ("c", 0, 0), ("c", 0, 1), ("e",), ("c", 0, 2), ("c", 0, 3), ("c", 0, 4), ("c", 0, 5), ("c", 0, 6), ("c", 0, 7),
    ("c", 1, 0), ("c", 1, 1), ("c", 1, 2), ("c", 1, 7), ("c", 1, 3), ("c", 1, 4), ("c", 1, 5), ("c", 1, 6),
)
LOADS = (
    ("c", 0, 0, 1), ("w", 0), ("w", 1), ("c", 0, 1, 1), ("c", 0, 2, 1), ("e",), ("c", 0, 3, 1),
    ("c", 0, 4, 2), ("c", 0, 6, 2), ("c", 1, 0, 2), ("c", 1, 2, 2), ("c", 1, 4, 2), ("c", 1, 6, 2),
)
QUEUE = (
    (0, 0), (0, 1), (0, 2), "e", (0, 3), (0, 4), (0, 5), (0, 6), (0, 7),
    (1, 0), (1, 1), (1, 2), (1, 6), (1, 7), (1, 3), (1, 4), (1, 5),
)
FRONT = 1
SHIFT = 1
WARM = (8, 2)
V_P0 = 6
V_P1 = 5
QK = 4
RK = 5
GB = 3
G_SHARE = (0, 0, 5, 4, 3, 3)
EAGER_ITEMS = (0,)
HALVED = 2
LAST_G = 1


def tile_gcn_layer_t_kernel(tc, x, weight, grad_out, out):
    nc = tc.nc
    with ExitStack() as ctx:
        ctx.enter_context(tc.manual_schedule())
        const = ctx.enter_context(tc.tile_pool(name="const", bufs=1))
        raws = ctx.enter_context(tc.tile_pool(name="raws", bufs=1))
        grp = ctx.enter_context(tc.tile_pool(name="grp", bufs=GB))
        evens = ctx.enter_context(tc.tile_pool(name="evens", bufs=8))
        small = ctx.enter_context(tc.tile_pool(name="small", bufs=4))
        eds = ctx.enter_context(tc.tile_pool(name="eds", bufs=4))
        outs = ctx.enter_context(tc.tile_pool(name="outs", bufs=4))
        psum = ctx.enter_context(tc.psum_pool(name="psum", bufs=8))

        g_flat = grad_out.rearrange("b (p t) i j -> b p t (i j)", t=4)
        g_rows = grad_out.rearrange("b (p t) i j -> b p t i j", t=4)
        out_v = out.rearrange("b (ct c) i j -> b c ct (i j)", c=P)
        w_v = weight[0].rearrange("(ct c) o -> c ct o", c=P)

        row0 = {}
        rows = {}
        piece = {}
        unit_of = {}
        for b in range(B):
            r = 0
            for j, nr in enumerate(ROWS[b]):
                row0[(b, j)] = r
                rows[(b, j)] = nr
                piece[(b, j)] = (r + SHIFT * (j > 0), min(r + nr + SHIFT, SIDE))
                r += nr
            j0 = 0
            for n in UNITS[b]:
                for j in range(j0, j0 + n):
                    unit_of[(b, j)] = (b, j0, n)
                j0 += n

        def need(item):
            if item[0] == "e":
                return ["e"]
            b, j = item[1:]
            return [(b, i) for i in range(max(j - 1, 0), min(j + 2 - SHIFT, len(ROWS[b])))]

        w_raw = raws.tile([P, CT, C], BF16, name="w_raw")
        src = {}

        def load_w(half):
            nc.sync.dma_start(out=w_raw[:, 2 * half : 2 * half + 2, :], in_=w_v[:, 2 * half : 2 * half + 2, :])

        def load(b, j, n):
            r0 = piece[(b, j)][0]
            r1 = piece[(b, j + n - 1)][1]
            raw = raws.tile([P, 4, (r1 - r0) * SIDE], BF16, name="raw_%d_%d" % (b, j))
            nc.sync.dma_start(out=raw[:], in_=g_flat[b, :, :, r0 * SIDE : r1 * SIDE])
            for i in range(j, j + n):
                q0, q1 = piece[(b, i)]
                src[(b, i)] = raw[:, :, (q0 - r0) * SIDE : (q1 - r0) * SIDE]

        for spec in LOADS:
            if spec[0] == "w":
                load_w(spec[1])
            elif spec[0] == "e":
                raw_e = raws.tile([P, 4, 2 * B, SIDE], BF16, name="raw_e")
                for b in range(B):
                    for e in range(2):
                        nc.sync.dma_start(out=raw_e[:, :, 2 * b + e, :], in_=g_rows[b, :, :, e * (SIDE - 1), :])
                src["e"] = raw_e[:].rearrange("p t r j -> p t (r j)")
            else:
                load(*spec[1:])

        ident = const.tile([P, P], F32)
        make_identity(nc, ident[:])
        padded = (FRONT + SIDE + 1) * SIDE
        codes = const.tile([P, B, padded], U32, align_bytes=64)
        scales = const.tile([P, B, padded], U8, align_bytes=64)
        e_span = 2 * B * SIDE
        e_codes = const.tile([P, 3 * e_span], U32, align_bytes=64)
        e_scales = const.tile([P, 3 * e_span], U8, align_bytes=64)
        w_codes = const.tile([P, C], U32, align_bytes=64)
        w_scales = const.tile([P, C], U8, align_bytes=64)
        nc.vector.memset(codes[:, :, 0 : FRONT * SIDE].bitcast(I32), 0)
        nc.vector.memset(codes[:, :, padded - SIDE : padded].bitcast(I32), 0)
        nc.vector.memset(scales[:, :, 0 : FRONT * SIDE].bitcast(I32), 0)
        nc.vector.memset(scales[:, :, padded - SIDE : padded].bitcast(I32), 0)
        for z in (0, 2 * e_span):
            nc.vector.memset(e_codes[:, z : z + e_span].bitcast(I32), 0)
            nc.vector.memset(e_scales[:, z : z + e_span].bitcast(I32), 0)

        grouped_w = const.tile([P, 4 * C], BF16, align_bytes=64, name="grouped_w")
        w32 = w_raw[:].bitcast(F32)
        gw32 = grouped_w[:].bitcast(F32).rearrange("p (ct c h) -> p ct c h", ct=CT, h=2)

        def transpose_w(half):
            w_t = psum.tile([P, BANK], F32, tag="bank", name="w_t%d" % half)
            w_tv = w_t[:].rearrange("p (c2 h c) -> p c2 h c", c2=2, h=2)
            for c2 in range(2):
                for h in range(2):
                    nc.tensor.transpose(w_tv[:, c2, h, :], w32[:, 2 * half + c2, h : C // 2 : 2], ident[:])
            nc.scalar.copy(out=gw32[:, 2 * half : 2 * half + 2, :, :], in_=w_tv.rearrange("p c2 h c -> p c2 c h"))

        def quantise_w(half):
            nc.vector.quantize_mx(
                out=w_codes[:, half * 2 * P : (half + 1) * 2 * P].bitcast(E4X4),
                scales=w_scales[:, half * 2 * P : (half + 1) * 2 * P],
                in_=grouped_w[:, half * 2 * C : (half + 1) * 2 * C],
            )

        dummy = const.tile([P, BANK], BF16)
        nc.vector.memset(dummy[:], 0.0)

        def warm_up(count):
            for n in range(count):
                bank = psum.tile([P, BANK], F32, tag="bank", name="dummy_%d_%d" % (count, n))
                nc.tensor.matmul(out=bank[:], lhsT=dummy[:, 0:P], rhs=dummy[:], start=True, stop=True)

        grouped_of = {}

        def move_on_gpsimd(out, in_):
            nc.gpsimd.tensor_scalar(out=out, in0=in_, scalar1=1.0, scalar2=0.0, op0=ALU.mult, op1=ALU.add)

        def regroup(bj, shares):
            n = 2 * B if bj == "e" else piece[bj][1] - piece[bj][0]
            grouped = grp.tile(
                [P, 4 * (SLOTS + 1) * SIDE], BF16, align_bytes=64, tag="grouped", name="grouped_%s_%s" % (bj[0], bj[-1])
            )
            grouped_of[bj] = grouped
            r = 0
            for copy, nr in shares:
                nr = min(nr, n - r)
                if nr == 0:
                    continue
                s = src[bj][:, :, r * SIDE : (r + nr) * SIDE]
                d = grouped[:, r * 4 * SIDE : (r + nr) * 4 * SIDE]
                if copy == "gpsimd":
                    move_on_gpsimd(
                        d.rearrange("p (a s t) -> p a s t", s=2, t=4),
                        s.rearrange("p t (a s) -> p a s t", s=2)[:, :, ::-1, :],
                    )
                else:
                    (nc.vector.tensor_copy if copy == "vector" else nc.scalar.copy)(
                        out=d.rearrange("p (a s t) -> p a t s", s=2, t=4),
                        in_=s.rearrange("p t (a s) -> p a t s", s=2)[:, :, :, ::-1],
                    )
                r += nr

        done = []

        def quantise(bj):
            if bj in done:
                return
            done.append(bj)
            grouped = grouped_of[bj]
            if bj == "e":
                nc.vector.quantize_mx(
                    out=e_codes[:, e_span : 2 * e_span].bitcast(E5X4),
                    scales=e_scales[:, e_span : 2 * e_span],
                    in_=grouped[:, 0 : 4 * e_span],
                )
                return
            b = bj[0]
            r, r1 = piece[bj]
            at = 0
            for n in (8, 4, 2, 1):
                if r + n <= r1:
                    c0 = (FRONT + r) * SIDE
                    nc.vector.quantize_mx(
                        out=codes[:, b, c0 : c0 + n * SIDE].bitcast(E5X4),
                        scales=scales[:, b, c0 : c0 + n * SIDE],
                        in_=grouped[:, at * 4 * SIDE : (at + n) * 4 * SIDE],
                    )
                    r += n
                    at += n

        work = {}

        def banks_of(item):
            return 2 if item[0] == "e" else CT

        def width_of(item):
            return BANK if item[0] == "e" else rows[item[1:]] * SIDE

        def factor_of(item):
            return (U - 1.0) * NINTH if item[0] == "e" else NINTH

        def name_of(item):
            return "_".join([str(v) for v in item])

        def stage_m(item, ct):
            for bj in need(item):
                assert bj in done
            bank = psum.tile([P, BANK], F32, tag="bank", name="bank_%s_%d" % (name_of(item), ct))
            windows = []
            if item[0] == "e":
                off = 0
                for n, c0 in enumerate((e_span, 0)):
                    windows.append((2 * ct + n, e_codes[:, c0 : c0 + BANK], e_scales[:, c0 : c0 + BANK]))
            else:
                b, j = item[1:]
                off = BANK - rows[(b, j)] * SIDE
                for d in (-1, 0, 1):
                    c0 = (FRONT + row0[(b, j)] + d) * SIDE - off
                    windows.append((ct, codes[:, b, c0 : c0 + BANK], scales[:, b, c0 : c0 + BANK]))
            for n, (wt, rhs, rhs_scale) in enumerate(windows):
                nc.tensor.matmul_mx(
                    out=bank[:],
                    lhsT=w_codes[:, wt * P : (wt + 1) * P].bitcast(E4X4),
                    lhsT_scale=w_scales[:, wt * P : (wt + 1) * P],
                    rhs=rhs.bitcast(E5X4),
                    rhs_scale=rhs_scale,
                    start=(n == 0),
                    stop=(n == len(windows) - 1),
                )
            work[(item, ct)] = {"x": bank[:, off : off + width_of(item)]}

        out_of = {}
        ed_of = {}

        def group_of(item):
            if item[0] == "e":
                return item, 0, width_of(item) // SIDE
            b, j0, n = unit_of[item[1:]]
            return (b, j0), row0[item[1:]] - row0[(b, j0)], sum(ROWS[b][j0 : j0 + n])

        def out_rows(item, ct):
            key, at, total = group_of(item)
            if key not in out_of:
                if item[0] == "e":
                    o_new = raws.tile([P, 2, total * SIDE], F32, name="extra")
                else:
                    o_new = outs.tile([P, CT, total * SIDE], F32, tag="o", name="o_" + name_of(item))
                out_of[key] = o_new
            return out_of[key][:, ct, at * SIDE : at * SIDE + width_of(item)]

        def stage_e(item, ct):
            key, at, total = group_of(item)
            if key not in ed_of:
                ed_new = eds.tile([P, banks_of(item), total, 4], F32, tag="ed", name="ed_" + name_of(item))
                ed_of[key] = ed_new
            width = width_of(item)
            n = width // SIDE
            xv = work[(item, ct)]["x"]
            nc.scalar.activation(
                out=ed_of[key][:, ct, at : at + n, :].rearrange("p r (s k) -> p r s k", k=2),
                in_=xv.rearrange("p (r s k) -> p r s k", s=HALF, k=2)[:, :, 0 : HALF : HALF - 1, :],
                func=ACT.Copy,
                scale=U * factor_of(item),
            )
            even = evens.tile([P, BANK // 2], F32, tag="even", name="even_%s_%d" % (name_of(item), ct))
            nc.scalar.activation(out=even[:, 0 : width // 2], in_=xv[:, 1:width:2], func=ACT.Copy, scale=factor_of(item))
            work[(item, ct)]["even"] = even

        def stage_p(item, ct):
            width = width_of(item)
            m = width // 2 - 1
            pair = small.tile([P, BANK // 2], F32, tag="pair", name="pair_%s_%d" % (name_of(item), ct))
            nc.vector.scalar_tensor_tensor(
                out=pair[:, 0:m],
                in0=work[(item, ct)]["x"][:, 0 : width - 2 : 2],
                scalar=factor_of(item),
                in1=work[(item, ct)]["even"][:, 1 : width // 2],
                op0=ALU.mult,
                op1=ALU.add,
            )
            work[(item, ct)]["pair"] = pair

        def stage_h(item, ct):
            width = width_of(item)
            m = width // 2 - 1
            nc.vector.scalar_tensor_tensor(
                out=out_rows(item, ct)[:, 1 : width - 1].rearrange("p (m e) -> p m e", e=2),
                in0=work[(item, ct)]["x"][:, 1 : width - 1].rearrange("p (m e) -> p m e", e=2),
                scalar=factor_of(item),
                in1=work[(item, ct)]["pair"][:, 0:m].unsqueeze(2).to_broadcast([P, m, 2]),
                op0=ALU.mult,
                op1=ALU.add,
            )

        def column_edges(on_vector, n, o3, ed3):
            edge = ed3[:, :, 1:3]
            inner = ed3[:, :, 0:4:3]
            next_cols = o3[:, :, 1 : SIDE - 1 : SIDE - 3]
            edge_cols = o3[:, :, 0 : SIDE : SIDE - 1]
            if on_vector:
                nc.vector.scalar_tensor_tensor(
                    out=next_cols, in0=edge, scalar=(U - 1.0) / U, in1=next_cols, op0=ALU.mult, op1=ALU.add
                )
                nc.vector.scalar_tensor_tensor(out=edge_cols, in0=edge, scalar=U, in1=inner, op0=ALU.mult, op1=ALU.add)
            else:
                t1 = small.tile([P, n, 2], F32, tag="t1", name="t1")
                t2 = small.tile([P, n, 2], F32, tag="t2", name="t2")
                nc.gpsimd.tensor_scalar(out=t1[:], in0=edge, scalar1=(U - 1.0) / U, scalar2=0.0, op0=ALU.mult, op1=ALU.add)
                nc.gpsimd.tensor_scalar(out=t2[:], in0=edge, scalar1=U, scalar2=0.0, op0=ALU.mult, op1=ALU.add)
                nc.gpsimd.tensor_tensor(out=next_cols, in0=next_cols, in1=t1[:], op=ALU.add)
                nc.gpsimd.tensor_tensor(out=edge_cols, in0=t2[:], in1=inner, op=ALU.add)

        def fix_columns(on_vector, key, ct0, nct):
            o = out_of[key][:, ct0 : ct0 + nct, :]
            n = nct * o.shape[2] // SIDE
            column_edges(
                on_vector,
                n,
                o.rearrange("p ct (r j) -> p (ct r) j", j=SIDE),
                ed_of[key][:, ct0 : ct0 + nct, :, :].rearrange("p ct r k -> p (ct r) k"),
            )

        def border_rows(key, ct0, nct):
            b, j0 = key
            n = unit_of[key][2]
            first = row0[key]
            last = first + sum(ROWS[b][j0 : j0 + n]) - 1
            o4 = out_of[key][:, ct0 : ct0 + nct, :].rearrange("p ct (r j) -> p ct r j", j=SIDE)
            for row, r0 in ((0, 0), (SIDE - 1, last - first - 1)):
                if not first <= row <= last:
                    continue
                at = 0 if row == 0 else last - first
                ex4 = out_of[("e",)][:].rearrange("p h (ct r j) -> p (h ct) r j", ct=2, j=SIDE)
                i = 2 * b + (row > 0)
                two = o4[:, :, r0 : r0 + 2, :]
                nc.gpsimd.tensor_tensor(
                    out=two,
                    in0=two,
                    in1=ex4[:, ct0 : ct0 + nct, i, :].unsqueeze(2).to_broadcast([P, nct, 2, SIDE]),
                    op=ALU.add,
                )
                nc.gpsimd.tensor_scalar(
                    out=o4[:, :, at, :], in0=o4[:, :, at, :], scalar1=U, scalar2=0.0, op0=ALU.mult, op1=ALU.add
                )

        def store(key, ct0, nct):
            b, j0 = key
            r0 = row0[key]
            r1 = r0 + sum(ROWS[b][j0 : j0 + unit_of[key][2]])
            nc.sync.dma_start(
                out=out_v[b, :, ct0 : ct0 + nct, r0 * SIDE : r1 * SIDE], in_=out_of[key][:, ct0 : ct0 + nct, :]
            )

        waiting = []

        def ready(key):
            b, j0 = key
            inside = j0 > 0 and j0 + unit_of[key][2] < len(ROWS[b])
            return inside or ("e",) in finished

        finished = []

        def finish(item):
            finished.append(item)
            if item[0] == "e":
                fix_columns(False, item, 0, 2)
            else:
                b, j0, n = unit_of[item[1:]]
                if item[2] != j0 + n - 1:
                    return
                fix_columns(False, (b, j0), 0, CT)
                waiting.append((b, j0))
            for key in list(waiting):
                if ready(key):
                    waiting.remove(key)
                    border_rows(key, 0, CT)
                    store(key, 0, CT)

        def finish_part(item, ct0, nct, on_vector):
            key = item[1:]
            assert unit_of[key][1:] == (key[1], 1) and ready(key)
            fix_columns(on_vector, key, ct0, nct)
            border_rows(key, ct0, nct)
            store(key, ct0, nct)

        n_items = len(ORDER)
        place = {"regroup": 0, "quantise": 0}

        def advance(kind, call, count):
            while place[kind] < min(count, len(QUEUE)):
                call(QUEUE[place[kind]])
                place[kind] += 1

        def regroup_next(bj):
            if bj == "e":
                regroup(bj, (("gpsimd", 2 * B),))
            elif bj in QUEUE[0:2]:
                regroup(bj, (("vector", V_P0 if bj == QUEUE[0] else V_P1), ("scalar", SLOTS + 1)))
            else:
                n = QUEUE.index(bj)
                regroup(bj, (("gpsimd", G_SHARE[n] if n < len(G_SHARE) else 0), ("scalar", SLOTS + 1)))

        advance("regroup", regroup_next, 1)
        warm_up(WARM[0])
        transpose_w(0)
        transpose_w(1)
        warm_up(WARM[1])
        advance("quantise", quantise, 1)
        quantise_w(0)
        advance("regroup", regroup_next, 2)
        quantise_w(1)
        advance("quantise", quantise, 2)
        for i in range(-1, n_items):
            item = ORDER[i] if i >= 0 else None
            follower = ORDER[i + 1] if i + 1 < n_items else None
            if follower:
                for ct in range(banks_of(follower)):
                    stage_m(follower, ct)
                    stage_e(follower, ct)
            advance("regroup", regroup_next, i + RK)
            last = i == n_items - 1
            halves = n_items - 1 - HALVED <= i < n_items - 1
            n_banks = banks_of(item) if item else 0
            if last:
                for n in range(CT):
                    if n < 2:
                        stage_p(item, n + 1)
                    stage_h(item, n)
                    if n == 2:
                        stage_p(item, 3)
                    finish_part(item, n, 1, n >= LAST_G)
                break
            eager = i in EAGER_ITEMS
            for n in range(max(n_banks, 1)):
                if eager:
                    if n > 0:
                        stage_p(item, n)
                    if n == n_banks - 1:
                        advance("quantise", quantise, i + QK)
                        stage_p(follower, 0)
                elif n + 1 < n_banks:
                    stage_p(item, n + 1)
                else:
                    if item:
                        advance("quantise", quantise, i + QK)
                    if follower:
                        stage_p(follower, 0)
                if n < n_banks:
                    stage_h(item, n)
                    if halves and n % 2 == 1:
                        finish_part(item, n - 1, 2, False)
            if item and not halves:
                finish(item)
